import numpy as np
import ml_dtypes


def mxq(x, axis, fmt="e4m3"):
    dtype, down = {"e4m3": (ml_dtypes.float8_e4m3fn, 7), "e5m2": (ml_dtypes.float8_e5m2, 14)}[fmt]
    v = np.moveaxis(np.asarray(x, np.float32).astype(ml_dtypes.bfloat16).astype(np.float64), axis, -1)
    blocks = v.reshape(v.shape[:-1] + (-1, 32))
    amax = np.abs(blocks).max(-1, keepdims=True)
    byte = np.maximum(np.where(amax > 0, np.frexp(amax)[1] - 1 + 127, 0) - down, 1)
    scale = np.exp2(byte - 127.0)
    codes = (blocks / scale).astype(np.float32).astype(dtype).astype(np.float64)
    return np.moveaxis((codes * scale).reshape(v.shape), -1, axis)


WIDE = False


def mx_kscale(k):
    if not WIDE:
        return np.ones(k)
    levels = np.array([10, -10, 5, -5, 0])
    a = np.random.permutation(np.resize(levels, k // 512 * 4)).reshape(k // 512, 4)
    idx = np.arange(k)
    return np.exp2(a[idx // 512, idx % 128 // 32])


BF16 = ml_dtypes.bfloat16


def bf(x):
    return np.asarray(x, np.float32).astype(BF16)


def f64(x):
    return np.asarray(x).astype(np.float64)


B, N, IN_DIM, OUT_DIM, K = 4, 1024, 1024, 128, 3
EPS = 1e-6
SIG = 2.0


def laplacian(adj):
    d = adj.sum(axis=2)
    r = (d + EPS) ** -0.5
    return np.eye(N)[None] - r[:, :, None] * adj * r[:, None, :]


def setup_inputs():
    s, u = mx_kscale(N), mx_kscale(IN_DIM)
    sn = s / s.max()
    return {"x": bf(np.random.standard_normal((B, N, IN_DIM)) * sn[:, None] * u),
            "tx1": bf(np.random.standard_normal((B, N, IN_DIM)) * sn[:, None] * u),
            "adj": bf(np.exp(SIG * np.random.standard_normal((B, N, N)) - SIG * SIG / 2.0) / N * (s * s)[:, None]),
            "W": bf(np.random.standard_normal((K, IN_DIM, OUT_DIM)) / np.sqrt(IN_DIM) / u[:, None]),
            "b": bf(np.random.standard_normal((K, OUT_DIM)) * 0.3)}


def reference(x, tx1, adj, W, b):
    x, tx1, b = f64(x), f64(tx1), f64(b)
    Wq = mxq(f64(W), 1, "e4m3")
    L = laplacian(f64(adj))
    out = (mxq(x, 2, "e4m3") @ Wq[0]) + b[0] + (mxq(tx1, 2, "e4m3") @ Wq[1]) + b[1]
    tx2 = 2.0 * (mxq(L, 2, "e4m3") @ mxq(tx1, 1, "e4m3")) - x
    out = out + (mxq(tx2, 2, "e4m3") @ Wq[2]) + b[2]
    return np.maximum(out, 0.0)

@@ -1,0 +1,316 @@
+from contextlib import ExitStack
+
+import concourse.mybir as mybir
+from concourse.masks import make_identity
+
+F32 = mybir.dt.float32
+BF16 = mybir.dt.bfloat16
+U32 = mybir.dt.uint32
+U8 = mybir.dt.uint8
+FP8X4 = mybir.dt.float8_e4m3fn_x4
+ALU = mybir.AluOpType
+ACT = mybir.ActivationFunctionType
+
+P = 128
+GRAPHS = 4
+NODES = 1024
+FEATS = 1024
+OUT = 128
+ORDERS = 3
+EPS = 1e-6
+
+PACK = 4
+K_PASS = P * PACK
+PASSES = NODES // K_PASS
+CHUNKS = NODES // P
+HALF = CHUNKS // PASSES
+ALL_CHUNKS = GRAPHS * CHUNKS
+
+AHEAD_MX1 = 1
+AHEAD_T = 2
+AHEAD_PREP = AHEAD_T + CHUNKS + 1
+AHEAD_LOAD = AHEAD_PREP + HALF
+
+FLOPS = GRAPHS * (2 * NODES * NODES * FEATS + ORDERS * 2 * NODES * FEATS * OUT)
+
+
+def tile_cheblayer_pb_t_kernel(tc, x, tx1, adj, W, b, out):
+    nc = tc.nc
+    with ExitStack() as stack:
+        pool = lambda name, bufs: stack.enter_context(tc.tile_pool(name=name, bufs=bufs))
+        const = pool("const", 1)
+        adj_pool = pool("adj", 4)
+        tx1_pool = pool("tx1", 4)
+        x_pool = pool("x", 3)
+        graph_pool = pool("graph", 3)
+        node_pool = pool("node", 5)
+        stage = pool("stage", 3)
+        chunk_pool = pool("chunk", 4)
+        psum_t = stack.enter_context(tc.psum_pool(name="psum_t", bufs=3))
+        psum_m = stack.enter_context(tc.psum_pool(name="psum_m", bufs=2))
+        psum_o = stack.enter_context(tc.psum_pool(name="psum_o", bufs=2))
+        psum_f = stack.enter_context(tc.psum_pool(name="psum_f", bufs=1))
+
+        ident = const.tile([P, P], F32)
+        make_identity(nc, ident[:])
+        ident_bf = const.tile([P, P], BF16)
+        make_identity(nc, ident_bf[:])
+        eps = const.tile([P, 1], F32)
+        nc.vector.memset(eps[:], EPS)
+        warm = const.tile([P, 1], F32)
+        nc.scalar.activation(out=warm[:], in_=eps[:], func=ACT.Sqrt)
+
+        halves = {}
+
+        def load_half(name, src, tile_pool, g, h):
+            t = tile_pool.tile([P, HALF, FEATS], BF16, name=name)
+            nc.sync.dma_start(
+                out=t[:].rearrange("p (c e) f -> p c e f", e=2),
+                in_=src[g, h * K_PASS : (h + 1) * K_PASS, :].rearrange("(c p e) f -> p c e f", p=P, e=2),
+            )
+            halves[(name, g, h)] = t
+
+        def load_for(q):
+            if q % HALF == 0 and CHUNKS <= q < ALL_CHUNKS:
+                g, h = q // CHUNKS, (q % CHUNKS) // HALF
+                load_half("adj", adj, adj_pool, g, h)
+                load_half("tx1", tx1, tx1_pool, g, h)
+
+        def load_x_for(q):
+            if q % HALF == 0 and HALF <= q < ALL_CHUNKS:
+                load_half("x", x, x_pool, q // CHUNKS, (q % CHUNKS) // HALF)
+
+        w_raw = const.tile([P, ORDERS * PASSES, PACK, OUT], BF16)
+        w_grouped = const.tile([P, ORDERS * PASSES, OUT, PACK], BF16, align_bytes=64)
+        w_codes = const.tile([P, ORDERS, PASSES, OUT], U32, align_bytes=64)
+        w_scales = const.tile([P, ORDERS, PASSES, OUT], U8, align_bytes=64)
+        b_rows = const.tile([P, ORDERS, OUT], BF16)
+        bias01 = const.tile([P, OUT], F32)
+        bias = const.tile([P, OUT], F32)
+
+        def prepare_weights():
+            nc.sync.dma_start(
+                out=w_raw[:].rearrange("p a (u e) o -> p (a u) e o", e=2),
+                in_=W.rearrange("k (a p e) o -> p (k a) e o", p=P, e=2),
+            )
+            nc.sync.dma_start(
+                out=b_rows[:].rearrange("p k o -> p (k o)"),
+                in_=b.rearrange("k o -> (k o)").partition_broadcast(P),
+            )
+            nc.vector.tensor_copy(out=w_grouped[:], in_=w_raw[:].rearrange("p a t o -> p a o t"))
+            for k in range(ORDERS):
+                nc.vector.quantize_mx(
+                    out=w_codes[:, k].rearrange("p a o -> p (a o)").bitcast(FP8X4),
+                    scales=w_scales[:, k].rearrange("p a o -> p (a o)"),
+                    in_=w_grouped[:, k * PASSES : (k + 1) * PASSES].rearrange("p a o t -> p (a o t)"),
+                )
+            nc.vector.tensor_tensor(out=bias01[:], in0=b_rows[:, 0, :], in1=b_rows[:, 1, :], op=ALU.add)
+            nc.vector.tensor_tensor(out=bias[:], in0=bias01[:], in1=b_rows[:, 2, :], op=ALU.add)
+
+        vectors = {}
+        node_codes = {}
+
+        def prepare(q):
+            g, k = q // CHUNKS, q % CHUNKS
+            h, j = k // HALF, k % HALF
+            if k == 0:
+                vectors[g] = {"d": graph_pool.tile([P, CHUNKS], F32, name="d")}
+            folded = psum_f.tile([P, P], F32, name="folded")
+            for blk in range(CHUNKS):
+                nc.tensor.matmul(
+                    out=folded[:],
+                    lhsT=ident_bf[:],
+                    rhs=halves[("adj", g, h)][:, j, blk * P : (blk + 1) * P],
+                    start=(blk == 0),
+                    stop=(blk == CHUNKS - 1),
+                )
+            junk = stage.tile([P, P], F32, name="junk")
+            nc.scalar.activation(
+                out=junk[:], in_=folded[:], func=ACT.Copy, accum_out=vectors[g]["d"][:, k : k + 1]
+            )
+
+            if j == 0:
+                node_codes[(g, h)] = (
+                    node_pool.tile([P, FEATS], U32, name="node_c", align_bytes=64),
+                    node_pool.tile([P, FEATS], U8, name="node_s", align_bytes=64),
+                )
+            window = slice(j * 2 * P, (j + 1) * 2 * P)
+            node_grouped = stage.tile([P, 2, P, PACK], BF16, name="node_grouped", align_bytes=64)
+            rows = halves[("tx1", g, h)][:, :, window].rearrange("p t (m e) -> p e m t", e=2)
+            if g == 0:
+                nc.vector.tensor_copy(out=node_grouped[:], in_=rows)
+            else:
+                nc.scalar.copy(out=node_grouped[:], in_=rows)
+            codes, scales = node_codes[(g, h)]
+            nc.vector.quantize_mx(
+                out=codes[:, window].bitcast(FP8X4),
+                scales=scales[:, window],
+                in_=node_grouped[:].rearrange("p e m t -> p (e m t)"),
+            )
+            if k == CHUNKS - 1:
+                finish_vectors(g)
+
+        def finish_vectors(g):
+            v = vectors[g]
+            root = graph_pool.tile([P, CHUNKS], F32, name="root")
+            nc.scalar.activation(out=root[:], in_=v["d"][:], func=ACT.Sqrt, bias=eps[:, 0:1])
+            v["r"] = graph_pool.tile([P, CHUNKS], F32, name="r")
+            nc.vector.reciprocal(out=v["r"][:], in_=root[:])
+            v["neg_r"] = graph_pool.tile([P, CHUNKS], F32, name="neg_r")
+            nc.vector.tensor_scalar_mul(out=v["neg_r"][:], in0=v["r"][:], scalar1=-1.0)
+            v["r_cols"] = graph_pool.tile([P, NODES], F32, name="r_cols")
+            for h in range(PASSES):
+                spread = psum_t.tile([P, HALF, P], F32, name="bank")
+                for j in range(HALF):
+                    k = h * HALF + j
+                    nc.tensor.transpose(
+                        out=spread[:, j, :], in_=v["r"][:, k : k + 1].to_broadcast([P, P]), identity=ident[:]
+                    )
+                nc.scalar.copy(
+                    out=v["r_cols"][:, h * K_PASS : (h + 1) * K_PASS].rearrange("p (c n e) -> p c n e", n=P, e=2),
+                    in_=spread[:].rearrange("p (c e) n -> p c n e", e=2),
+                )
+
+        chunks = {}
+
+        def transposed_words(src_half, j):
+            words = src_half[:].bitcast(F32)
+            bank = psum_t.tile([P, PACK, P], F32, name="bank")
+            for u in range(PACK):
+                nc.tensor.transpose(out=bank[:, u, :], in_=words[:, j, u * P : (u + 1) * P], identity=ident[:])
+            return bank
+
+        def stage_transpose(s):
+            g, k = s // CHUNKS, s % CHUNKS
+            h, j = k // HALF, k % HALF
+            c, e = k // 2, k % 2
+            v = vectors[g]
+            t = {}
+            chunks[s] = t
+
+            row = halves[("adj", g, h)][:, j, :]
+            neg_r = v["neg_r"][:, k : k + 1]
+            diag_cols = lambda ap: ap.rearrange("p (w n e) -> p w n e", n=P, e=2)[:, c, :, e]
+            diag = stage.tile([P, P], F32, name="diag")
+            nc.vector.scalar_tensor_tensor(
+                out=diag[:], in0=diag_cols(row), scalar=neg_r, in1=diag_cols(v["r_cols"][:]), op0=ALU.mult, op1=ALU.mult
+            )
+            nc.vector.scalar_tensor_tensor(
+                out=row, in0=row, scalar=neg_r, in1=v["r_cols"][:], op0=ALU.mult, op1=ALU.mult
+            )
+            nc.vector.tensor_tensor(out=diag_cols(row), in0=diag[:], in1=ident[:], op=ALU.add)
+
+            t["feat_grouped"] = chunk_pool.tile([P, 2, PASSES, P, PACK], BF16, name="feat_grouped", align_bytes=64)
+            feat_words = t["feat_grouped"][:].bitcast(F32)
+            for m, name in enumerate(("x", "tx1")):
+                bank = transposed_words(halves[(name, g, h)], j)
+                nc.scalar.copy(out=feat_words[:, m], in_=bank[:].rearrange("p (a u) i -> p a i u", u=2))
+            t["feat_c"] = chunk_pool.tile([P, 2, PASSES, P], U32, name="feat_c", align_bytes=64)
+            t["feat_s"] = chunk_pool.tile([P, 2, PASSES, P], U8, name="feat_s", align_bytes=64)
+            nc.vector.quantize_mx(
+                out=t["feat_c"][:].rearrange("p m a i -> p (m a i)").bitcast(FP8X4),
+                scales=t["feat_s"][:].rearrange("p m a i -> p (m a i)"),
+                in_=t["feat_grouped"][:].rearrange("p m a i t -> p (m a i t)"),
+            )
+
+            bank = transposed_words(halves[("adj", g, h)], j)
+            pairs = bank[:].bitcast(BF16).rearrange("p (a u) (i e) -> p a i u e", u=2, e=2)
+            lap_grouped = stage.tile([P, PASSES, P, PACK], BF16, name="lap_grouped", align_bytes=64)
+            for a in range(PASSES):
+                nc.scalar.copy(out=lap_grouped[:, a].rearrange("p i (u e) -> p i u e", e=2), in_=pairs[:, a])
+            t["lap_c"] = chunk_pool.tile([P, PASSES, P], U32, name="lap_c", align_bytes=64)
+            t["lap_s"] = chunk_pool.tile([P, PASSES, P], U8, name="lap_s", align_bytes=64)
+            nc.vector.quantize_mx(
+                out=t["lap_c"][:].rearrange("p a i -> p (a i)").bitcast(FP8X4),
+                scales=t["lap_s"][:].rearrange("p a i -> p (a i)"),
+                in_=lap_grouped[:].rearrange("p a i t -> p (a i t)"),
+            )
+
+        def stage_second_order(s):
+            g = s // CHUNKS
+            t = chunks[s]
+            tx2_grouped = stage.tile([P, PASSES, P, PACK], BF16, name="tx2_grouped", align_bytes=64)
+            for a in range(PASSES):
+                acc = psum_m.tile([P, PACK, P], F32, name="acc")
+                for v in range(PACK):
+                    cols = slice((a * PACK + v) * P, (a * PACK + v + 1) * P)
+                    for h in range(PASSES):
+                        codes, scales = node_codes[(g, h)]
+                        nc.tensor.matmul_mx(
+                            out=acc[:, v, :],
+                            lhsT=codes[:, cols].bitcast(FP8X4),
+                            lhsT_scale=scales[:, cols],
+                            rhs=t["lap_c"][:, h, :].bitcast(FP8X4),
+                            rhs_scale=t["lap_s"][:, h, :],
+                            start=(h == 0),
+                            stop=(h == PASSES - 1),
+                        )
+                nc.vector.scalar_tensor_tensor(
+                    out=tx2_grouped[:, a],
+                    in0=acc[:].rearrange("p v i -> p i v"),
+                    scalar=2.0,
+                    in1=t["feat_grouped"][:, 0, a],
+                    op0=ALU.mult,
+                    op1=ALU.subtract,
+                )
+            t["tx2_c"] = chunk_pool.tile([P, PASSES, P], U32, name="tx2_c", align_bytes=64)
+            t["tx2_s"] = chunk_pool.tile([P, PASSES, P], U8, name="tx2_s", align_bytes=64)
+            nc.vector.quantize_mx(
+                out=t["tx2_c"][:].rearrange("p a i -> p (a i)").bitcast(FP8X4),
+                scales=t["tx2_s"][:].rearrange("p a i -> p (a i)"),
+                in_=tx2_grouped[:].rearrange("p a i t -> p (a i t)"),
+            )
+
+        pair_acc = {}
+
+        def stage_output(s):
+            g, k = s // CHUNKS, s % CHUNKS
+            c, e = k // 2, k % 2
+            t = chunks[s]
+            if e == 0:
+                pair_acc[0] = psum_o.tile([P, 2, OUT], F32, name="out_acc")
+            out_acc = pair_acc[0]
+            operands = [
+                (t["feat_c"][:, 0], t["feat_s"][:, 0]),
+                (t["feat_c"][:, 1], t["feat_s"][:, 1]),
+                (t["tx2_c"][:], t["tx2_s"][:]),
+            ]
+            for k_order, (codes, scales) in enumerate(operands):
+                for a in range(PASSES):
+                    nc.tensor.matmul_mx(
+                        out=out_acc[:, e, :],
+                        lhsT=codes[:, a, :].bitcast(FP8X4),
+                        lhsT_scale=scales[:, a, :],
+                        rhs=w_codes[:, k_order, a, :].bitcast(FP8X4),
+                        rhs_scale=w_scales[:, k_order, a, :],
+                        start=(k_order == 0 and a == 0),
+                        stop=(k_order == ORDERS - 1 and a == PASSES - 1),
+                    )
+            if e == 1:
+                summed = stage.tile([P, 2, OUT], F32, name="summed")
+                nc.vector.tensor_tensor(
+                    out=summed[:], in0=out_acc[:], in1=bias[:].unsqueeze(1).to_broadcast([P, 2, OUT]), op=ALU.add
+                )
+                result = stage.tile([P, 2, OUT], F32, name="result")
+                nc.scalar.activation(out=result[:], in_=summed[:], func=ACT.Relu)
+                nc.gpsimd.dma_start(
+                    out=out[g, c * 2 * P : (c + 1) * 2 * P, :].rearrange("(p e) o -> p e o", e=2), in_=result[:]
+                )
+
+        for h in range(PASSES):
+            load_half("adj", adj, adj_pool, 0, h)
+        for h in range(PASSES):
+            load_half("tx1", tx1, tx1_pool, 0, h)
+        load_half("x", x, x_pool, 0, 0)
+        prepare_weights()
+        for s in range(-AHEAD_PREP, ALL_CHUNKS):
+            if s >= 0:
+                stage_output(s)
+            if 0 <= s + AHEAD_MX1 < ALL_CHUNKS:
+                stage_second_order(s + AHEAD_MX1)
+            if 0 <= s + AHEAD_T < ALL_CHUNKS:
+                stage_transpose(s + AHEAD_T)
+            if 0 <= s + AHEAD_PREP < ALL_CHUNKS:
+                prepare(s + AHEAD_PREP)
+            load_for(s + AHEAD_LOAD)
+            load_x_for(s + AHEAD_PREP)

@@ -26,10 +26,25 @@ CHUNKS = NODES // P
 HALF = CHUNKS // PASSES
 ALL_CHUNKS = GRAPHS * CHUNKS
 
-AHEAD_MX1 = 1
-AHEAD_T = 2
-AHEAD_PREP = AHEAD_T + CHUNKS + 1
-AHEAD_LOAD = AHEAD_PREP + HALF
+AT_STORE = 0
+AT_OUTPUT = 1
+AT_TERM = 2
+AT_SECOND_ORDER = 3
+AT_QUANTISE = 4
+AT_TRANSPOSE = 5
+AT_LAP = 6
+AT_SPREAD = 7
+AT_ROOT = 8
+AT_ROW_SUMS = AT_ROOT + CHUNKS
+AT_NODE_QUANTISE = AT_SECOND_ORDER + 1 + CHUNKS
+AT_NODE_REGROUP = AT_NODE_QUANTISE + 1
+LOAD_AHEAD = 4
+ADJ_BUFS = 5
+TX1_BUFS = 4
+X_BUFS = 2
+assert AT_ROW_SUMS + LOAD_AHEAD <= AT_TRANSPOSE + (ADJ_BUFS - 1) * HALF
+assert AT_NODE_REGROUP + LOAD_AHEAD <= AT_TRANSPOSE + (TX1_BUFS - 1) * HALF
+assert AT_TRANSPOSE + LOAD_AHEAD <= AT_TRANSPOSE + (X_BUFS - 1) * HALF
 
 FLOPS = GRAPHS * (2 * NODES * NODES * FEATS + ORDERS * 2 * NODES * FEATS * OUT)
 
@@ -39,17 +54,18 @@ def tile_cheblayer_pb_t_kernel(tc, x, tx1, adj, W, b, out):
     with ExitStack() as stack:
         pool = lambda name, bufs: stack.enter_context(tc.tile_pool(name=name, bufs=bufs))
         const = pool("const", 1)
-        adj_pool = pool("adj", 4)
-        tx1_pool = pool("tx1", 4)
-        x_pool = pool("x", 3)
+        adj_pool = pool("adj", ADJ_BUFS)
+        tx1_pool = pool("tx1", TX1_BUFS)
+        x_pool = pool("x", X_BUFS)
         graph_pool = pool("graph", 3)
         node_pool = pool("node", 5)
-        stage = pool("stage", 3)
-        chunk_pool = pool("chunk", 4)
+        short = pool("short", 3)
+        long = pool("long", 5)
         psum_t = stack.enter_context(tc.psum_pool(name="psum_t", bufs=3))
         psum_m = stack.enter_context(tc.psum_pool(name="psum_m", bufs=2))
         psum_o = stack.enter_context(tc.psum_pool(name="psum_o", bufs=2))
         psum_f = stack.enter_context(tc.psum_pool(name="psum_f", bufs=1))
+        stack.enter_context(tc.manual_schedule())
 
         ident = const.tile([P, P], F32)
         make_identity(nc, ident[:])
@@ -62,7 +78,8 @@ def tile_cheblayer_pb_t_kernel(tc, x, tx1, adj, W, b, out):
 
         halves = {}
 
-        def load_half(name, src, tile_pool, g, h):
+        def load_half(name, src, tile_pool, q):
+            g, h = q // CHUNKS, (q % CHUNKS) // HALF
             t = tile_pool.tile([P, HALF, FEATS], BF16, name=name)
             nc.sync.dma_start(
                 out=t[:].rearrange("p (c e) f -> p c e f", e=2),
@@ -70,15 +87,8 @@ def tile_cheblayer_pb_t_kernel(tc, x, tx1, adj, W, b, out):
             )
             halves[(name, g, h)] = t
 
-        def load_for(q):
-            if q % HALF == 0 and CHUNKS <= q < ALL_CHUNKS:
-                g, h = q // CHUNKS, (q % CHUNKS) // HALF
-                load_half("adj", adj, adj_pool, g, h)
-                load_half("tx1", tx1, tx1_pool, g, h)
-
-        def load_x_for(q):
-            if q % HALF == 0 and HALF <= q < ALL_CHUNKS:
-                load_half("x", x, x_pool, q // CHUNKS, (q % CHUNKS) // HALF)
+        def half_of(name, s):
+            return halves[(name, s // CHUNKS, (s % CHUNKS) // HALF)]
 
         w_raw = const.tile([P, ORDERS * PASSES, PACK, OUT], BF16)
         w_grouped = const.tile([P, ORDERS * PASSES, OUT, PACK], BF16, align_bytes=64)
@@ -88,7 +98,7 @@ def tile_cheblayer_pb_t_kernel(tc, x, tx1, adj, W, b, out):
         bias01 = const.tile([P, OUT], F32)
         bias = const.tile([P, OUT], F32)
 
-        def prepare_weights():
+        def load_weights():
             nc.sync.dma_start(
                 out=w_raw[:].rearrange("p a (u e) o -> p (a u) e o", e=2),
                 in_=W.rearrange("k (a p e) o -> p (k a) e o", p=P, e=2),
@@ -97,22 +107,47 @@ def tile_cheblayer_pb_t_kernel(tc, x, tx1, adj, W, b, out):
                 out=b_rows[:].rearrange("p k o -> p (k o)"),
                 in_=b.rearrange("k o -> (k o)").partition_broadcast(P),
             )
+
+        def quantise_weights():
             nc.vector.tensor_copy(out=w_grouped[:], in_=w_raw[:].rearrange("p a t o -> p a o t"))
+            nc.vector.tensor_tensor(out=bias01[:], in0=b_rows[:, 0, :], in1=b_rows[:, 1, :], op=ALU.add)
             for k in range(ORDERS):
                 nc.vector.quantize_mx(
                     out=w_codes[:, k].rearrange("p a o -> p (a o)").bitcast(FP8X4),
                     scales=w_scales[:, k].rearrange("p a o -> p (a o)"),
                     in_=w_grouped[:, k * PASSES : (k + 1) * PASSES].rearrange("p a o t -> p (a o t)"),
                 )
-            nc.vector.tensor_tensor(out=bias01[:], in0=b_rows[:, 0, :], in1=b_rows[:, 1, :], op=ALU.add)
             nc.vector.tensor_tensor(out=bias[:], in0=bias01[:], in1=b_rows[:, 2, :], op=ALU.add)
 
         vectors = {}
         node_codes = {}
+        node_grouped = {}
 
-        def prepare(q):
+        def window_of(q):
+            j = q % HALF
+            return slice(j * 2 * P, (j + 1) * 2 * P)
+
+        def node_regroup(q):
+            node_grouped[q] = short.tile([P, 2, P, PACK], BF16, name="node_grouped", align_bytes=64)
+            rows = half_of("tx1", q)[:, :, window_of(q)].rearrange("p t (m e) -> p e m t", e=2)
+            nc.scalar.copy(out=node_grouped[q][:], in_=rows)
+
+        def node_quantise(q):
+            key = (q // CHUNKS, (q % CHUNKS) // HALF)
+            if q % HALF == 0:
+                node_codes[key] = (
+                    node_pool.tile([P, FEATS], U32, name="node_c", align_bytes=64),
+                    node_pool.tile([P, FEATS], U8, name="node_s", align_bytes=64),
+                )
+            codes, scales = node_codes[key]
+            nc.vector.quantize_mx(
+                out=codes[:, window_of(q)].bitcast(FP8X4),
+                scales=scales[:, window_of(q)],
+                in_=node_grouped[q][:].rearrange("p e m t -> p (e m t)"),
+            )
+
+        def row_sums(q):
             g, k = q // CHUNKS, q % CHUNKS
-            h, j = k // HALF, k % HALF
             if k == 0:
                 vectors[g] = {"d": graph_pool.tile([P, CHUNKS], F32, name="d")}
             folded = psum_f.tile([P, P], F32, name="folded")
@@ -120,44 +155,26 @@ def tile_cheblayer_pb_t_kernel(tc, x, tx1, adj, W, b, out):
                 nc.tensor.matmul(
                     out=folded[:],
                     lhsT=ident_bf[:],
-                    rhs=halves[("adj", g, h)][:, j, blk * P : (blk + 1) * P],
+                    rhs=half_of("adj", q)[:, q % HALF, blk * P : (blk + 1) * P],
                     start=(blk == 0),
                     stop=(blk == CHUNKS - 1),
                 )
-            junk = stage.tile([P, P], F32, name="junk")
-            nc.scalar.activation(
-                out=junk[:], in_=folded[:], func=ACT.Copy, accum_out=vectors[g]["d"][:, k : k + 1]
-            )
+            junk = short.tile([P, P], F32, name="junk")
+            nc.scalar.activation(out=junk[:], in_=folded[:], func=ACT.Copy, accum_out=vectors[g]["d"][:, k : k + 1])
 
-            if j == 0:
-                node_codes[(g, h)] = (
-                    node_pool.tile([P, FEATS], U32, name="node_c", align_bytes=64),
-                    node_pool.tile([P, FEATS], U8, name="node_s", align_bytes=64),
-                )
-            window = slice(j * 2 * P, (j + 1) * 2 * P)
-            node_grouped = stage.tile([P, 2, P, PACK], BF16, name="node_grouped", align_bytes=64)
-            rows = halves[("tx1", g, h)][:, :, window].rearrange("p t (m e) -> p e m t", e=2)
-            if g == 0:
-                nc.vector.tensor_copy(out=node_grouped[:], in_=rows)
-            else:
-                nc.scalar.copy(out=node_grouped[:], in_=rows)
-            codes, scales = node_codes[(g, h)]
-            nc.vector.quantize_mx(
-                out=codes[:, window].bitcast(FP8X4),
-                scales=scales[:, window],
-                in_=node_grouped[:].rearrange("p e m t -> p (e m t)"),
-            )
-            if k == CHUNKS - 1:
-                finish_vectors(g)
+        def vectors_root(g):
+            vectors[g]["root"] = graph_pool.tile([P, CHUNKS], F32, name="root")
+            nc.scalar.activation(out=vectors[g]["root"][:], in_=vectors[g]["d"][:], func=ACT.Sqrt, bias=eps[:, 0:1])
 
-        def finish_vectors(g):
+        def vectors_reciprocal(g):
             v = vectors[g]
-            root = graph_pool.tile([P, CHUNKS], F32, name="root")
-            nc.scalar.activation(out=root[:], in_=v["d"][:], func=ACT.Sqrt, bias=eps[:, 0:1])
             v["r"] = graph_pool.tile([P, CHUNKS], F32, name="r")
-            nc.vector.reciprocal(out=v["r"][:], in_=root[:])
+            nc.vector.reciprocal(out=v["r"][:], in_=v["root"][:])
             v["neg_r"] = graph_pool.tile([P, CHUNKS], F32, name="neg_r")
             nc.vector.tensor_scalar_mul(out=v["neg_r"][:], in0=v["r"][:], scalar1=-1.0)
+
+        def vectors_spread(g):
+            v = vectors[g]
             v["r_cols"] = graph_pool.tile([P, NODES], F32, name="r_cols")
             for h in range(PASSES):
                 spread = psum_t.tile([P, HALF, P], F32, name="bank")
@@ -171,7 +188,7 @@ def tile_cheblayer_pb_t_kernel(tc, x, tx1, adj, W, b, out):
                     in_=spread[:].rearrange("p (c e) n -> p c n e", e=2),
                 )
 
-        chunks = {}
+        chunks = {s: {} for s in range(ALL_CHUNKS)}
 
         def transposed_words(src_half, j):
             words = src_half[:].bitcast(F32)
@@ -180,62 +197,74 @@ def tile_cheblayer_pb_t_kernel(tc, x, tx1, adj, W, b, out):
                 nc.tensor.transpose(out=bank[:, u, :], in_=words[:, j, u * P : (u + 1) * P], identity=ident[:])
             return bank
 
-        def stage_transpose(s):
-            g, k = s // CHUNKS, s % CHUNKS
-            h, j = k // HALF, k % HALF
-            c, e = k // 2, k % 2
-            v = vectors[g]
-            t = {}
-            chunks[s] = t
-
-            row = halves[("adj", g, h)][:, j, :]
-            neg_r = v["neg_r"][:, k : k + 1]
-            diag_cols = lambda ap: ap.rearrange("p (w n e) -> p w n e", n=P, e=2)[:, c, :, e]
-            diag = stage.tile([P, P], F32, name="diag")
-            nc.vector.scalar_tensor_tensor(
-                out=diag[:], in0=diag_cols(row), scalar=neg_r, in1=diag_cols(v["r_cols"][:]), op0=ALU.mult, op1=ALU.mult
-            )
-            nc.vector.scalar_tensor_tensor(
-                out=row, in0=row, scalar=neg_r, in1=v["r_cols"][:], op0=ALU.mult, op1=ALU.mult
-            )
-            nc.vector.tensor_tensor(out=diag_cols(row), in0=diag[:], in1=ident[:], op=ALU.add)
-
-            t["feat_grouped"] = chunk_pool.tile([P, 2, PASSES, P, PACK], BF16, name="feat_grouped", align_bytes=64)
+        def feat_transpose(s):
+            t = chunks[s]
+            t["feat_grouped"] = long.tile([P, 2, PASSES, P, PACK], BF16, name="feat_grouped", align_bytes=64)
             feat_words = t["feat_grouped"][:].bitcast(F32)
             for m, name in enumerate(("x", "tx1")):
-                bank = transposed_words(halves[(name, g, h)], j)
+                bank = transposed_words(half_of(name, s), s % HALF)
                 nc.scalar.copy(out=feat_words[:, m], in_=bank[:].rearrange("p (a u) i -> p a i u", u=2))
-            t["feat_c"] = chunk_pool.tile([P, 2, PASSES, P], U32, name="feat_c", align_bytes=64)
-            t["feat_s"] = chunk_pool.tile([P, 2, PASSES, P], U8, name="feat_s", align_bytes=64)
+
+        def feat_quantise(s):
+            t = chunks[s]
+            t["feat_c"] = long.tile([P, 2, PASSES, P], U32, name="feat_c", align_bytes=64)
+            t["feat_s"] = long.tile([P, 2, PASSES, P], U8, name="feat_s", align_bytes=64)
             nc.vector.quantize_mx(
                 out=t["feat_c"][:].rearrange("p m a i -> p (m a i)").bitcast(FP8X4),
                 scales=t["feat_s"][:].rearrange("p m a i -> p (m a i)"),
                 in_=t["feat_grouped"][:].rearrange("p m a i t -> p (m a i t)"),
             )
 
-            bank = transposed_words(halves[("adj", g, h)], j)
+        def lap_operands(s):
+            k = s % CHUNKS
+            v = vectors[s // CHUNKS]
+            diag_cols = lambda ap: ap.rearrange("p (w n e) -> p w n e", n=P, e=2)[:, k // 2, :, k % 2]
+            return half_of("adj", s)[:, s % HALF, :], v["neg_r"][:, k : k + 1], v["r_cols"][:], diag_cols
+
+        def lap_diagonal(s):
+            row, neg_r, r_cols, diag_cols = lap_operands(s)
+            chunks[s]["diag"] = short.tile([P, P], F32, name="diag")
+            nc.vector.scalar_tensor_tensor(
+                out=chunks[s]["diag"][:], in0=diag_cols(row), scalar=neg_r, in1=diag_cols(r_cols), op0=ALU.mult, op1=ALU.mult
+            )
+
+        def lap_rows(s):
+            row, neg_r, r_cols, diag_cols = lap_operands(s)
+            nc.vector.scalar_tensor_tensor(out=row, in0=row, scalar=neg_r, in1=r_cols, op0=ALU.mult, op1=ALU.mult)
+
+        def lap_add_eye(s):
+            row, neg_r, r_cols, diag_cols = lap_operands(s)
+            nc.vector.tensor_tensor(out=diag_cols(row), in0=chunks[s]["diag"][:], in1=ident[:], op=ALU.add)
+
+        def lap_transpose(s):
+            bank = transposed_words(half_of("adj", s), s % HALF)
             pairs = bank[:].bitcast(BF16).rearrange("p (a u) (i e) -> p a i u e", u=2, e=2)
-            lap_grouped = stage.tile([P, PASSES, P, PACK], BF16, name="lap_grouped", align_bytes=64)
+            chunks[s]["lap_grouped"] = short.tile([P, PASSES, P, PACK], BF16, name="lap_grouped", align_bytes=64)
             for a in range(PASSES):
-                nc.scalar.copy(out=lap_grouped[:, a].rearrange("p i (u e) -> p i u e", e=2), in_=pairs[:, a])
-            t["lap_c"] = chunk_pool.tile([P, PASSES, P], U32, name="lap_c", align_bytes=64)
-            t["lap_s"] = chunk_pool.tile([P, PASSES, P], U8, name="lap_s", align_bytes=64)
+                nc.scalar.copy(
+                    out=chunks[s]["lap_grouped"][:, a].rearrange("p i (u e) -> p i u e", e=2), in_=pairs[:, a]
+                )
+
+        def lap_quantise(s):
+            t = chunks[s]
+            t["lap_c"] = short.tile([P, PASSES, P], U32, name="lap_c", align_bytes=64)
+            t["lap_s"] = short.tile([P, PASSES, P], U8, name="lap_s", align_bytes=64)
             nc.vector.quantize_mx(
                 out=t["lap_c"][:].rearrange("p a i -> p (a i)").bitcast(FP8X4),
                 scales=t["lap_s"][:].rearrange("p a i -> p (a i)"),
-                in_=lap_grouped[:].rearrange("p a i t -> p (a i t)"),
+                in_=t["lap_grouped"][:].rearrange("p a i t -> p (a i t)"),
             )
 
-        def stage_second_order(s):
-            g = s // CHUNKS
+        def second_order_products(s):
             t = chunks[s]
-            tx2_grouped = stage.tile([P, PASSES, P, PACK], BF16, name="tx2_grouped", align_bytes=64)
+            t["acc"] = []
             for a in range(PASSES):
                 acc = psum_m.tile([P, PACK, P], F32, name="acc")
+                t["acc"].append(acc)
                 for v in range(PACK):
                     cols = slice((a * PACK + v) * P, (a * PACK + v + 1) * P)
                     for h in range(PASSES):
-                        codes, scales = node_codes[(g, h)]
+                        codes, scales = node_codes[(s // CHUNKS, h)]
                         nc.tensor.matmul_mx(
                             out=acc[:, v, :],
                             lhsT=codes[:, cols].bitcast(FP8X4),
@@ -245,72 +274,127 @@ def tile_cheblayer_pb_t_kernel(tc, x, tx1, adj, W, b, out):
                             start=(h == 0),
                             stop=(h == PASSES - 1),
                         )
-                nc.vector.scalar_tensor_tensor(
-                    out=tx2_grouped[:, a],
-                    in0=acc[:].rearrange("p v i -> p i v"),
-                    scalar=2.0,
-                    in1=t["feat_grouped"][:, 0, a],
-                    op0=ALU.mult,
-                    op1=ALU.subtract,
-                )
-            t["tx2_c"] = chunk_pool.tile([P, PASSES, P], U32, name="tx2_c", align_bytes=64)
-            t["tx2_s"] = chunk_pool.tile([P, PASSES, P], U8, name="tx2_s", align_bytes=64)
+
+        def second_order_term(s, a):
+            t = chunks[s]
+            if a == 0:
+                t["tx2_grouped"] = short.tile([P, PASSES, P, PACK], BF16, name="tx2_grouped", align_bytes=64)
+            nc.vector.scalar_tensor_tensor(
+                out=t["tx2_grouped"][:, a],
+                in0=t["acc"][a][:].rearrange("p v i -> p i v"),
+                scalar=2.0,
+                in1=t["feat_grouped"][:, 0, a],
+                op0=ALU.mult,
+                op1=ALU.subtract,
+            )
+
+        def tx2_quantise(s):
+            t = chunks[s]
+            t["tx2_c"] = short.tile([P, PASSES, P], U32, name="tx2_c", align_bytes=64)
+            t["tx2_s"] = short.tile([P, PASSES, P], U8, name="tx2_s", align_bytes=64)
             nc.vector.quantize_mx(
                 out=t["tx2_c"][:].rearrange("p a i -> p (a i)").bitcast(FP8X4),
                 scales=t["tx2_s"][:].rearrange("p a i -> p (a i)"),
-                in_=tx2_grouped[:].rearrange("p a i t -> p (a i t)"),
+                in_=t["tx2_grouped"][:].rearrange("p a i t -> p (a i t)"),
             )
 
         pair_acc = {}
 
-        def stage_output(s):
-            g, k = s // CHUNKS, s % CHUNKS
-            c, e = k // 2, k % 2
+        def output_products(s):
             t = chunks[s]
-            if e == 0:
-                pair_acc[0] = psum_o.tile([P, 2, OUT], F32, name="out_acc")
-            out_acc = pair_acc[0]
+            if s % 2 == 0:
+                pair_acc[s // 2] = psum_o.tile([P, 2, OUT], F32, name="out_acc")
             operands = [
                 (t["feat_c"][:, 0], t["feat_s"][:, 0]),
                 (t["feat_c"][:, 1], t["feat_s"][:, 1]),
                 (t["tx2_c"][:], t["tx2_s"][:]),
             ]
-            for k_order, (codes, scales) in enumerate(operands):
+            for k, (codes, scales) in enumerate(operands):
                 for a in range(PASSES):
                     nc.tensor.matmul_mx(
-                        out=out_acc[:, e, :],
+                        out=pair_acc[s // 2][:, s % 2, :],
                         lhsT=codes[:, a, :].bitcast(FP8X4),
                         lhsT_scale=scales[:, a, :],
-                        rhs=w_codes[:, k_order, a, :].bitcast(FP8X4),
-                        rhs_scale=w_scales[:, k_order, a, :],
-                        start=(k_order == 0 and a == 0),
-                        stop=(k_order == ORDERS - 1 and a == PASSES - 1),
+                        rhs=w_codes[:, k, a, :].bitcast(FP8X4),
+                        rhs_scale=w_scales[:, k, a, :],
+                        start=(k == 0 and a == 0),
+                        stop=(k == ORDERS - 1 and a == PASSES - 1),
                     )
-            if e == 1:
-                summed = stage.tile([P, 2, OUT], F32, name="summed")
-                nc.vector.tensor_tensor(
-                    out=summed[:], in0=out_acc[:], in1=bias[:].unsqueeze(1).to_broadcast([P, 2, OUT]), op=ALU.add
-                )
-                result = stage.tile([P, 2, OUT], F32, name="result")
-                nc.scalar.activation(out=result[:], in_=summed[:], func=ACT.Relu)
-                nc.gpsimd.dma_start(
-                    out=out[g, c * 2 * P : (c + 1) * 2 * P, :].rearrange("(p e) o -> p e o", e=2), in_=result[:]
-                )
 
-        for h in range(PASSES):
-            load_half("adj", adj, adj_pool, 0, h)
-        for h in range(PASSES):
-            load_half("tx1", tx1, tx1_pool, 0, h)
-        load_half("x", x, x_pool, 0, 0)
-        prepare_weights()
-        for s in range(-AHEAD_PREP, ALL_CHUNKS):
-            if s >= 0:
-                stage_output(s)
-            if 0 <= s + AHEAD_MX1 < ALL_CHUNKS:
-                stage_second_order(s + AHEAD_MX1)
-            if 0 <= s + AHEAD_T < ALL_CHUNKS:
-                stage_transpose(s + AHEAD_T)
-            if 0 <= s + AHEAD_PREP < ALL_CHUNKS:
-                prepare(s + AHEAD_PREP)
-            load_for(s + AHEAD_LOAD)
-            load_x_for(s + AHEAD_PREP)
+        def output_bias(s):
+            chunks[s]["summed"] = short.tile([P, 2, OUT], F32, name="summed")
+            nc.vector.tensor_tensor(
+                out=chunks[s]["summed"][:],
+                in0=pair_acc[s // 2][:],
+                in1=bias[:].unsqueeze(1).to_broadcast([P, 2, OUT]),
+                op=ALU.add,
+            )
+
+        def output_store(s):
+            g, c = s // CHUNKS, (s % CHUNKS) // 2
+            result = short.tile([P, 2, OUT], F32, name="result")
+            nc.scalar.activation(out=result[:], in_=chunks[s]["summed"][:], func=ACT.Relu)
+            nc.gpsimd.dma_start(
+                out=out[g, c * 2 * P : (c + 1) * 2 * P, :].rearrange("(p e) o -> p e o", e=2), in_=result[:]
+            )
+
+        valid = lambda s: 0 <= s < ALL_CHUNKS
+        first_of_half = lambda s: valid(s) and s % HALF == 0
+        first_of_graph = lambda s: valid(s) and s % CHUNKS == 0
+        second_of_pair = lambda s: valid(s) and s % 2 == 1
+
+        first_step = -(AT_ROW_SUMS + LOAD_AHEAD)
+        for n in range(first_step, ALL_CHUNKS - AT_STORE):
+            if first_of_half(n + AT_ROW_SUMS + LOAD_AHEAD):
+                load_half("adj", adj, adj_pool, n + AT_ROW_SUMS + LOAD_AHEAD)
+            if first_of_half(n + AT_NODE_REGROUP + LOAD_AHEAD):
+                load_half("tx1", tx1, tx1_pool, n + AT_NODE_REGROUP + LOAD_AHEAD)
+            if n + AT_NODE_REGROUP + LOAD_AHEAD == 1:
+                load_weights()
+            if first_of_half(n + AT_TRANSPOSE + LOAD_AHEAD):
+                load_half("x", x, x_pool, n + AT_TRANSPOSE + LOAD_AHEAD)
+
+            if first_of_graph(n + AT_ROOT):
+                vectors_root((n + AT_ROOT) // CHUNKS)
+            if valid(n + AT_NODE_REGROUP):
+                node_regroup(n + AT_NODE_REGROUP)
+
+            if valid(n + AT_OUTPUT):
+                output_products(n + AT_OUTPUT)
+            if first_of_graph(n + AT_SPREAD):
+                vectors_spread((n + AT_SPREAD) // CHUNKS)
+            if valid(n + AT_TRANSPOSE):
+                feat_transpose(n + AT_TRANSPOSE)
+            if valid(n + AT_ROW_SUMS):
+                row_sums(n + AT_ROW_SUMS)
+            if valid(n + AT_TRANSPOSE):
+                lap_transpose(n + AT_TRANSPOSE)
+
+            if n + AT_NODE_QUANTISE == HALF:
+                quantise_weights()
+            if valid(n + AT_LAP):
+                lap_diagonal(n + AT_LAP)
+                lap_rows(n + AT_LAP)
+            if valid(n + AT_QUANTISE):
+                lap_quantise(n + AT_QUANTISE)
+            if valid(n + AT_TERM):
+                second_order_term(n + AT_TERM, 0)
+            if valid(n + AT_LAP):
+                lap_add_eye(n + AT_LAP)
+            if valid(n + AT_TERM):
+                second_order_term(n + AT_TERM, 1)
+            if valid(n + AT_QUANTISE):
+                feat_quantise(n + AT_QUANTISE)
+            if valid(n + AT_TERM):
+                tx2_quantise(n + AT_TERM)
+            if valid(n + AT_NODE_QUANTISE):
+                node_quantise(n + AT_NODE_QUANTISE)
+            if second_of_pair(n + AT_STORE):
+                output_bias(n + AT_STORE)
+            if first_of_graph(n + AT_ROOT):
+                vectors_reciprocal((n + AT_ROOT) // CHUNKS)
+
+            if valid(n + AT_SECOND_ORDER):
+                second_order_products(n + AT_SECOND_ORDER)
+            if second_of_pair(n + AT_STORE):
+                output_store(n + AT_STORE)

@@ -19,6 +19,7 @@ OUT = 128
 ORDERS = 3
 EPS = 1e-6
 
+BLOCK_BF16 = 16
 PACK = 4
 K_PASS = P * PACK
 PASSES = NODES // K_PASS
@@ -26,20 +27,22 @@ CHUNKS = NODES // P
 HALF = CHUNKS // PASSES
 ALL_CHUNKS = GRAPHS * CHUNKS
 
-AT_STORE = 0
+AT_STORE = -1
+AT_RELU = 0
 AT_OUTPUT = 1
 AT_TERM = 2
 AT_SECOND_ORDER = 3
 AT_QUANTISE = 4
 AT_TRANSPOSE = 5
-AT_LAP = 6
-AT_SPREAD = 7
-AT_ROOT = 8
+AT_LAP = 12
+AT_SPREAD = AT_LAP + 1
+AT_RECIPROCAL = AT_LAP + 2
+AT_ROOT = AT_LAP + 3
 AT_ROW_SUMS = AT_ROOT + CHUNKS
 AT_NODE_QUANTISE = AT_SECOND_ORDER + 1 + CHUNKS
 AT_NODE_REGROUP = AT_NODE_QUANTISE + 1
 LOAD_AHEAD = 4
-ADJ_BUFS = 5
+ADJ_BUFS = 7
 TX1_BUFS = 4
 X_BUFS = 2
 assert AT_ROW_SUMS + LOAD_AHEAD <= AT_TRANSPOSE + (ADJ_BUFS - 1) * HALF
@@ -61,10 +64,9 @@ def tile_cheblayer_pb_t_kernel(tc, x, tx1, adj, W, b, out):
         node_pool = pool("node", 5)
         short = pool("short", 3)
         long = pool("long", 5)
-        psum_t = stack.enter_context(tc.psum_pool(name="psum_t", bufs=3))
+        psum_t = stack.enter_context(tc.psum_pool(name="psum_t", bufs=4))
         psum_m = stack.enter_context(tc.psum_pool(name="psum_m", bufs=2))
         psum_o = stack.enter_context(tc.psum_pool(name="psum_o", bufs=2))
-        psum_f = stack.enter_context(tc.psum_pool(name="psum_f", bufs=1))
         stack.enter_context(tc.manual_schedule())
 
         ident = const.tile([P, P], F32)
@@ -94,32 +96,31 @@ def tile_cheblayer_pb_t_kernel(tc, x, tx1, adj, W, b, out):
         w_grouped = const.tile([P, ORDERS * PASSES, OUT, PACK], BF16, align_bytes=64)
         w_codes = const.tile([P, ORDERS, PASSES, OUT], U32, align_bytes=64)
         w_scales = const.tile([P, ORDERS, PASSES, OUT], U8, align_bytes=64)
-        b_rows = const.tile([P, ORDERS, OUT], BF16)
-        bias01 = const.tile([P, OUT], F32)
-        bias = const.tile([P, OUT], F32)
+        b_rows = const.tile([P, P], BF16)
+        b_terms = const.tile([P, ORDERS], F32)
+        bias = const.tile([P, 1], F32)
 
         def load_weights():
             nc.sync.dma_start(
                 out=w_raw[:].rearrange("p a (u e) o -> p (a u) e o", e=2),
                 in_=W.rearrange("k (a p e) o -> p (k a) e o", p=P, e=2),
             )
-            nc.sync.dma_start(
-                out=b_rows[:].rearrange("p k o -> p (k o)"),
-                in_=b.rearrange("k o -> (k o)").partition_broadcast(P),
-            )
+            nc.vector.memset(b_rows[:], 0.0)
+            nc.sync.dma_start(out=b_rows[0:ORDERS, :], in_=b)
 
         def quantise_weights():
             nc.vector.tensor_copy(out=w_grouped[:], in_=w_raw[:].rearrange("p a t o -> p a o t"))
-            nc.vector.tensor_tensor(out=bias01[:], in0=b_rows[:, 0, :], in1=b_rows[:, 1, :], op=ALU.add)
             for k in range(ORDERS):
                 nc.vector.quantize_mx(
                     out=w_codes[:, k].rearrange("p a o -> p (a o)").bitcast(FP8X4),
                     scales=w_scales[:, k].rearrange("p a o -> p (a o)"),
                     in_=w_grouped[:, k * PASSES : (k + 1) * PASSES].rearrange("p a o t -> p (a o t)"),
                 )
-            nc.vector.tensor_tensor(out=bias[:], in0=bias01[:], in1=b_rows[:, 2, :], op=ALU.add)
+            b_cols = psum_t.tile([P, P], BF16, name="bank")
+            nc.tensor.transpose(out=b_cols[:], in_=b_rows[:], identity=ident_bf[:])
+            nc.scalar.activation(out=b_terms[:], in_=b_cols[:, 0:ORDERS], func=ACT.Copy, accum_out=bias[:, 0:1])
 
-        vectors = {}
+        vectors = {g: {} for g in range(GRAPHS)}
         node_codes = {}
         node_grouped = {}
 
@@ -149,8 +150,8 @@ def tile_cheblayer_pb_t_kernel(tc, x, tx1, adj, W, b, out):
         def row_sums(q):
             g, k = q // CHUNKS, q % CHUNKS
             if k == 0:
-                vectors[g] = {"d": graph_pool.tile([P, CHUNKS], F32, name="d")}
-            folded = psum_f.tile([P, P], F32, name="folded")
+                vectors[g]["d"] = graph_pool.tile([P, CHUNKS], F32, name="d")
+            folded = psum_t.tile([P, P], F32, name="bank")
             for blk in range(CHUNKS):
                 nc.tensor.matmul(
                     out=folded[:],
@@ -172,6 +173,35 @@ def tile_cheblayer_pb_t_kernel(tc, x, tx1, adj, W, b, out):
             nc.vector.reciprocal(out=v["r"][:], in_=v["root"][:])
             v["neg_r"] = graph_pool.tile([P, CHUNKS], F32, name="neg_r")
             nc.vector.tensor_scalar_mul(out=v["neg_r"][:], in0=v["r"][:], scalar1=-1.0)
+
+        def load_diagonal(g):
+            vectors[g]["a_diag"] = graph_pool.tile([P, 2, BLOCK_BF16], BF16, name="a_diag")
+            diagonal = adj[g].rearrange("i j -> (i j)")[0 : NODES * NODES : NODES + 1]
+            with nc.allow_non_contiguous_dma(reason="1,024 single elements, one from each row of adj"):
+                for e in range(2):
+                    nc.sync.dma_start(
+                        out=vectors[g]["a_diag"][:, e, 0 : CHUNKS // 2],
+                        in_=diagonal.rearrange("(c p e) -> p c e", p=P, e=2)[:, :, e],
+                    )
+
+        def vectors_diagonal(g):
+            v = vectors[g]
+            small = lambda name, dtype: graph_pool.tile([P, CHUNKS], dtype, name=name)
+            half_product, product, stored, one_more = (
+                small("half_product", F32), small("product", F32), small("stored", BF16), small("one_more", F32)
+            )
+            v["eye_fix"] = small("eye_fix", F32)
+            by_pair = lambda ap: ap.rearrange("p (c e) -> p c e", e=2)
+            nc.gpsimd.tensor_tensor(
+                out=by_pair(half_product[:]),
+                in0=v["a_diag"][:, :, 0 : CHUNKS // 2].rearrange("p e c -> p c e"),
+                in1=by_pair(v["neg_r"][:]),
+                op=ALU.mult,
+            )
+            nc.gpsimd.tensor_tensor(out=product[:], in0=half_product[:], in1=v["r"][:], op=ALU.mult)
+            nc.gpsimd.tensor_copy(out=stored[:], in_=product[:])
+            nc.gpsimd.tensor_scalar_add(out=one_more[:], in0=product[:], scalar1=1.0)
+            nc.gpsimd.tensor_tensor(out=v["eye_fix"][:], in0=one_more[:], in1=stored[:], op=ALU.subtract)
 
         def vectors_spread(g):
             v = vectors[g]
@@ -215,26 +245,26 @@ def tile_cheblayer_pb_t_kernel(tc, x, tx1, adj, W, b, out):
                 in_=t["feat_grouped"][:].rearrange("p m a i t -> p (m a i t)"),
             )
 
-        def lap_operands(s):
+        def lap_rows(s):
             k = s % CHUNKS
             v = vectors[s // CHUNKS]
-            diag_cols = lambda ap: ap.rearrange("p (w n e) -> p w n e", n=P, e=2)[:, k // 2, :, k % 2]
-            return half_of("adj", s)[:, s % HALF, :], v["neg_r"][:, k : k + 1], v["r_cols"][:], diag_cols
-
-        def lap_diagonal(s):
-            row, neg_r, r_cols, diag_cols = lap_operands(s)
-            chunks[s]["diag"] = short.tile([P, P], F32, name="diag")
+            row = half_of("adj", s)[:, s % HALF, :]
             nc.vector.scalar_tensor_tensor(
-                out=chunks[s]["diag"][:], in0=diag_cols(row), scalar=neg_r, in1=diag_cols(r_cols), op0=ALU.mult, op1=ALU.mult
+                out=row, in0=row, scalar=v["neg_r"][:, k : k + 1], in1=v["r_cols"][:], op0=ALU.mult, op1=ALU.mult
             )
 
-        def lap_rows(s):
-            row, neg_r, r_cols, diag_cols = lap_operands(s)
-            nc.vector.scalar_tensor_tensor(out=row, in0=row, scalar=neg_r, in1=r_cols, op0=ALU.mult, op1=ALU.mult)
-
         def lap_add_eye(s):
-            row, neg_r, r_cols, diag_cols = lap_operands(s)
-            nc.vector.tensor_tensor(out=diag_cols(row), in0=chunks[s]["diag"][:], in1=ident[:], op=ALU.add)
+            k = s % CHUNKS
+            row = half_of("adj", s)[:, s % HALF, :]
+            diag_cols = row.rearrange("p (w n e) -> p w n e", n=P, e=2)[:, k // 2, :, k % 2]
+            nc.vector.scalar_tensor_tensor(
+                out=diag_cols,
+                in0=ident[:],
+                scalar=vectors[s // CHUNKS]["eye_fix"][:, k : k + 1],
+                in1=diag_cols,
+                op0=ALU.mult,
+                op1=ALU.add,
+            )
 
         def lap_transpose(s):
             bank = transposed_words(half_of("adj", s), s % HALF)
@@ -303,7 +333,7 @@ def tile_cheblayer_pb_t_kernel(tc, x, tx1, adj, W, b, out):
         def output_products(s):
             t = chunks[s]
             if s % 2 == 0:
-                pair_acc[s // 2] = psum_o.tile([P, 2, OUT], F32, name="out_acc")
+                pair_acc[s // 2] = psum_o.tile([P, 2, P], F32, name="out_acc")
             operands = [
                 (t["feat_c"][:, 0], t["feat_s"][:, 0]),
                 (t["feat_c"][:, 1], t["feat_s"][:, 1]),
@@ -313,27 +343,25 @@ def tile_cheblayer_pb_t_kernel(tc, x, tx1, adj, W, b, out):
                 for a in range(PASSES):
                     nc.tensor.matmul_mx(
                         out=pair_acc[s // 2][:, s % 2, :],
-                        lhsT=codes[:, a, :].bitcast(FP8X4),
-                        lhsT_scale=scales[:, a, :],
-                        rhs=w_codes[:, k, a, :].bitcast(FP8X4),
-                        rhs_scale=w_scales[:, k, a, :],
+                        lhsT=w_codes[:, k, a, :].bitcast(FP8X4),
+                        lhsT_scale=w_scales[:, k, a, :],
+                        rhs=codes[:, a, :].bitcast(FP8X4),
+                        rhs_scale=scales[:, a, :],
                         start=(k == 0 and a == 0),
                         stop=(k == ORDERS - 1 and a == PASSES - 1),
                     )
 
-        def output_bias(s):
-            chunks[s]["summed"] = short.tile([P, 2, OUT], F32, name="summed")
-            nc.vector.tensor_tensor(
-                out=chunks[s]["summed"][:],
-                in0=pair_acc[s // 2][:],
-                in1=bias[:].unsqueeze(1).to_broadcast([P, 2, OUT]),
-                op=ALU.add,
-            )
+        def output_relu(s):
+            chunks[s]["relu"] = short.tile([P, 2, P], F32, name="relu")
+            nc.scalar.activation(out=chunks[s]["relu"][:], in_=pair_acc[s // 2][:], func=ACT.Relu, bias=bias[:, 0:1])
 
         def output_store(s):
             g, c = s // CHUNKS, (s % CHUNKS) // 2
+            bank = psum_t.tile([P, 2, OUT], F32, name="bank")
+            for e in range(2):
+                nc.tensor.transpose(out=bank[:, e, :], in_=chunks[s]["relu"][:, e, :], identity=ident[:])
             result = short.tile([P, 2, OUT], F32, name="result")
-            nc.scalar.activation(out=result[:], in_=chunks[s]["summed"][:], func=ACT.Relu)
+            nc.scalar.copy(out=result[:], in_=bank[:])
             nc.gpsimd.dma_start(
                 out=out[g, c * 2 * P : (c + 1) * 2 * P, :].rearrange("(p e) o -> p e o", e=2), in_=result[:]
             )
@@ -344,25 +372,32 @@ def tile_cheblayer_pb_t_kernel(tc, x, tx1, adj, W, b, out):
         second_of_pair = lambda s: valid(s) and s % 2 == 1
 
         first_step = -(AT_ROW_SUMS + LOAD_AHEAD)
+        load_weights()
         for n in range(first_step, ALL_CHUNKS - AT_STORE):
             if first_of_half(n + AT_ROW_SUMS + LOAD_AHEAD):
                 load_half("adj", adj, adj_pool, n + AT_ROW_SUMS + LOAD_AHEAD)
+            if first_of_graph(n + AT_ROW_SUMS):
+                load_diagonal((n + AT_ROW_SUMS) // CHUNKS)
             if first_of_half(n + AT_NODE_REGROUP + LOAD_AHEAD):
                 load_half("tx1", tx1, tx1_pool, n + AT_NODE_REGROUP + LOAD_AHEAD)
-            if n + AT_NODE_REGROUP + LOAD_AHEAD == 1:
-                load_weights()
             if first_of_half(n + AT_TRANSPOSE + LOAD_AHEAD):
                 load_half("x", x, x_pool, n + AT_TRANSPOSE + LOAD_AHEAD)
 
             if first_of_graph(n + AT_ROOT):
                 vectors_root((n + AT_ROOT) // CHUNKS)
+            if first_of_graph(n + AT_SPREAD):
+                vectors_spread((n + AT_SPREAD) // CHUNKS)
+                vectors_diagonal((n + AT_SPREAD) // CHUNKS)
+
+            if second_of_pair(n + AT_RELU):
+                output_relu(n + AT_RELU)
             if valid(n + AT_NODE_REGROUP):
                 node_regroup(n + AT_NODE_REGROUP)
 
             if valid(n + AT_OUTPUT):
                 output_products(n + AT_OUTPUT)
-            if first_of_graph(n + AT_SPREAD):
-                vectors_spread((n + AT_SPREAD) // CHUNKS)
+            if second_of_pair(n + AT_STORE):
+                output_store(n + AT_STORE)
             if valid(n + AT_TRANSPOSE):
                 feat_transpose(n + AT_TRANSPOSE)
             if valid(n + AT_ROW_SUMS):
@@ -370,10 +405,11 @@ def tile_cheblayer_pb_t_kernel(tc, x, tx1, adj, W, b, out):
             if valid(n + AT_TRANSPOSE):
                 lap_transpose(n + AT_TRANSPOSE)
 
-            if n + AT_NODE_QUANTISE == HALF:
+            if n == first_step:
                 quantise_weights()
+            if first_of_graph(n + AT_RECIPROCAL):
+                vectors_reciprocal((n + AT_RECIPROCAL) // CHUNKS)
             if valid(n + AT_LAP):
-                lap_diagonal(n + AT_LAP)
                 lap_rows(n + AT_LAP)
             if valid(n + AT_QUANTISE):
                 lap_quantise(n + AT_QUANTISE)
@@ -389,12 +425,6 @@ def tile_cheblayer_pb_t_kernel(tc, x, tx1, adj, W, b, out):
                 tx2_quantise(n + AT_TERM)
             if valid(n + AT_NODE_QUANTISE):
                 node_quantise(n + AT_NODE_QUANTISE)
-            if second_of_pair(n + AT_STORE):
-                output_bias(n + AT_STORE)
-            if first_of_graph(n + AT_ROOT):
-                vectors_reciprocal((n + AT_ROOT) // CHUNKS)
 
             if valid(n + AT_SECOND_ORDER):
                 second_order_products(n + AT_SECOND_ORDER)
-            if second_of_pair(n + AT_STORE):
-                output_store(n + AT_STORE)

@@ -34,15 +34,17 @@ AT_TERM = 2
 AT_SECOND_ORDER = 3
 AT_QUANTISE = 4
 AT_TRANSPOSE = 5
-AT_LAP = 12
+AT_EYE = 7
+AT_LAP = 8
 AT_SPREAD = AT_LAP + 1
 AT_RECIPROCAL = AT_LAP + 2
 AT_ROOT = AT_LAP + 3
 AT_ROW_SUMS = AT_ROOT + CHUNKS
 AT_NODE_QUANTISE = AT_SECOND_ORDER + 1 + CHUNKS
 AT_NODE_REGROUP = AT_NODE_QUANTISE + 1
+EARLY = 4
 LOAD_AHEAD = 4
-ADJ_BUFS = 7
+ADJ_BUFS = 6
 TX1_BUFS = 4
 X_BUFS = 2
 assert AT_ROW_SUMS + LOAD_AHEAD <= AT_TRANSPOSE + (ADJ_BUFS - 1) * HALF
@@ -131,7 +133,10 @@ def tile_cheblayer_pb_t_kernel(tc, x, tx1, adj, W, b, out):
         def node_regroup(q):
             node_grouped[q] = short.tile([P, 2, P, PACK], BF16, name="node_grouped", align_bytes=64)
             rows = half_of("tx1", q)[:, :, window_of(q)].rearrange("p t (m e) -> p e m t", e=2)
-            nc.scalar.copy(out=node_grouped[q][:], in_=rows)
+            if q < HALF:
+                nc.vector.tensor_copy(out=node_grouped[q][:], in_=rows)
+            else:
+                nc.scalar.copy(out=node_grouped[q][:], in_=rows)
 
         def node_quantise(q):
             key = (q // CHUNKS, (q % CHUNKS) // HALF)
@@ -257,14 +262,16 @@ def tile_cheblayer_pb_t_kernel(tc, x, tx1, adj, W, b, out):
             k = s % CHUNKS
             row = half_of("adj", s)[:, s % HALF, :]
             diag_cols = row.rearrange("p (w n e) -> p w n e", n=P, e=2)[:, k // 2, :, k % 2]
-            nc.vector.scalar_tensor_tensor(
-                out=diag_cols,
+            eye = short.tile([P, P], F32, name="eye")
+            nc.gpsimd.tensor_scalar(
+                out=eye[:],
                 in0=ident[:],
-                scalar=vectors[s // CHUNKS]["eye_fix"][:, k : k + 1],
-                in1=diag_cols,
+                scalar1=vectors[s // CHUNKS]["eye_fix"][:, k : k + 1],
+                scalar2=0.0,
                 op0=ALU.mult,
                 op1=ALU.add,
             )
+            nc.gpsimd.tensor_tensor(out=diag_cols, in0=diag_cols, in1=eye[:], op=ALU.add)
 
         def lap_transpose(s):
             bank = transposed_words(half_of("adj", s), s % HALF)
@@ -371,23 +378,29 @@ def tile_cheblayer_pb_t_kernel(tc, x, tx1, adj, W, b, out):
         first_of_graph = lambda s: valid(s) and s % CHUNKS == 0
         second_of_pair = lambda s: valid(s) and s % 2 == 1
 
-        first_step = -(AT_ROW_SUMS + LOAD_AHEAD)
-        load_weights()
+        def lap_side(m):
+            if m + EARLY < CHUNKS:
+                return m + EARLY
+            return m if m >= CHUNKS else -1
+
+        first_step = -(AT_ROW_SUMS + LOAD_AHEAD + EARLY)
         for n in range(first_step, ALL_CHUNKS - AT_STORE):
-            if first_of_half(n + AT_ROW_SUMS + LOAD_AHEAD):
-                load_half("adj", adj, adj_pool, n + AT_ROW_SUMS + LOAD_AHEAD)
-            if first_of_graph(n + AT_ROW_SUMS):
-                load_diagonal((n + AT_ROW_SUMS) // CHUNKS)
-            if first_of_half(n + AT_NODE_REGROUP + LOAD_AHEAD):
-                load_half("tx1", tx1, tx1_pool, n + AT_NODE_REGROUP + LOAD_AHEAD)
             if first_of_half(n + AT_TRANSPOSE + LOAD_AHEAD):
                 load_half("x", x, x_pool, n + AT_TRANSPOSE + LOAD_AHEAD)
+            if n + AT_TRANSPOSE + LOAD_AHEAD == 0:
+                load_weights()
+            if first_of_half(n + AT_NODE_REGROUP + LOAD_AHEAD):
+                load_half("tx1", tx1, tx1_pool, n + AT_NODE_REGROUP + LOAD_AHEAD)
+            if first_of_half(lap_side(n + AT_ROW_SUMS + LOAD_AHEAD)):
+                load_half("adj", adj, adj_pool, lap_side(n + AT_ROW_SUMS + LOAD_AHEAD))
+            if first_of_graph(lap_side(n + AT_ROW_SUMS)):
+                load_diagonal(lap_side(n + AT_ROW_SUMS) // CHUNKS)
 
-            if first_of_graph(n + AT_ROOT):
-                vectors_root((n + AT_ROOT) // CHUNKS)
-            if first_of_graph(n + AT_SPREAD):
-                vectors_spread((n + AT_SPREAD) // CHUNKS)
-                vectors_diagonal((n + AT_SPREAD) // CHUNKS)
+            if first_of_graph(lap_side(n + AT_ROOT)):
+                vectors_root(lap_side(n + AT_ROOT) // CHUNKS)
+            if first_of_graph(lap_side(n + AT_SPREAD)):
+                vectors_spread(lap_side(n + AT_SPREAD) // CHUNKS)
+                vectors_diagonal(lap_side(n + AT_SPREAD) // CHUNKS)
 
             if second_of_pair(n + AT_RELU):
                 output_relu(n + AT_RELU)
@@ -400,24 +413,21 @@ def tile_cheblayer_pb_t_kernel(tc, x, tx1, adj, W, b, out):
                 output_store(n + AT_STORE)
             if valid(n + AT_TRANSPOSE):
                 feat_transpose(n + AT_TRANSPOSE)
-            if valid(n + AT_ROW_SUMS):
-                row_sums(n + AT_ROW_SUMS)
+            if valid(lap_side(n + AT_ROW_SUMS)):
+                row_sums(lap_side(n + AT_ROW_SUMS))
             if valid(n + AT_TRANSPOSE):
                 lap_transpose(n + AT_TRANSPOSE)
 
-            if n == first_step:
+            if n + AT_QUANTISE == 0:
                 quantise_weights()
-            if first_of_graph(n + AT_RECIPROCAL):
-                vectors_reciprocal((n + AT_RECIPROCAL) // CHUNKS)
-            if valid(n + AT_LAP):
-                lap_rows(n + AT_LAP)
+            if first_of_graph(lap_side(n + AT_RECIPROCAL)):
+                vectors_reciprocal(lap_side(n + AT_RECIPROCAL) // CHUNKS)
+            if valid(lap_side(n + AT_LAP)):
+                lap_rows(lap_side(n + AT_LAP))
             if valid(n + AT_QUANTISE):
                 lap_quantise(n + AT_QUANTISE)
             if valid(n + AT_TERM):
                 second_order_term(n + AT_TERM, 0)
-            if valid(n + AT_LAP):
-                lap_add_eye(n + AT_LAP)
-            if valid(n + AT_TERM):
                 second_order_term(n + AT_TERM, 1)
             if valid(n + AT_QUANTISE):
                 feat_quantise(n + AT_QUANTISE)
@@ -425,6 +435,9 @@ def tile_cheblayer_pb_t_kernel(tc, x, tx1, adj, W, b, out):
                 tx2_quantise(n + AT_TERM)
             if valid(n + AT_NODE_QUANTISE):
                 node_quantise(n + AT_NODE_QUANTISE)
+
+            if valid(lap_side(n + AT_EYE)):
+                lap_add_eye(lap_side(n + AT_EYE))
 
             if valid(n + AT_SECOND_ORDER):
                 second_order_products(n + AT_SECOND_ORDER)

@@ -34,7 +34,6 @@ AT_TERM = 2
 AT_SECOND_ORDER = 3
 AT_QUANTISE = 4
 AT_TRANSPOSE = 5
-AT_EYE = 7
 AT_LAP = 8
 AT_SPREAD = AT_LAP + 1
 AT_RECIPROCAL = AT_LAP + 2
@@ -42,6 +41,8 @@ AT_ROOT = AT_LAP + 3
 AT_ROW_SUMS = AT_ROOT + CHUNKS
 AT_NODE_QUANTISE = AT_SECOND_ORDER + 1 + CHUNKS
 AT_NODE_REGROUP = AT_NODE_QUANTISE + 1
+X, TX1, LAP, TX2 = 0, 1, 2, 3
+TX2_LAG = AT_QUANTISE - AT_TERM
 EARLY = 4
 LOAD_AHEAD = 4
 ADJ_BUFS = 6
@@ -65,7 +66,8 @@ def tile_cheblayer_pb_t_kernel(tc, x, tx1, adj, W, b, out):
         graph_pool = pool("graph", 3)
         node_pool = pool("node", 5)
         short = pool("short", 3)
-        long = pool("long", 5)
+        grouped_pool = pool("grouped", 5)
+        codes_pool = pool("codes", 4)
         psum_t = stack.enter_context(tc.psum_pool(name="psum_t", bufs=4))
         psum_m = stack.enter_context(tc.psum_pool(name="psum_m", bufs=2))
         psum_o = stack.enter_context(tc.psum_pool(name="psum_o", bufs=2))
@@ -85,10 +87,9 @@ def tile_cheblayer_pb_t_kernel(tc, x, tx1, adj, W, b, out):
         def load_half(name, src, tile_pool, q):
             g, h = q // CHUNKS, (q % CHUNKS) // HALF
             t = tile_pool.tile([P, HALF, FEATS], BF16, name=name)
-            nc.sync.dma_start(
-                out=t[:].rearrange("p (c e) f -> p c e f", e=2),
-                in_=src[g, h * K_PASS : (h + 1) * K_PASS, :].rearrange("(c p e) f -> p c e f", p=P, e=2),
-            )
+            rows = src[g, h * K_PASS : (h + 1) * K_PASS, :].rearrange("(c p e) f -> c p e f", p=P, e=2)
+            for c in range(HALF // 2):
+                nc.sync.dma_start(out=t[:, 2 * c : 2 * c + 2, :], in_=rows[c])
             halves[(name, g, h)] = t
 
         def half_of(name, s):
@@ -126,30 +127,29 @@ def tile_cheblayer_pb_t_kernel(tc, x, tx1, adj, W, b, out):
         node_codes = {}
         node_grouped = {}
 
-        def window_of(q):
-            j = q % HALF
-            return slice(j * 2 * P, (j + 1) * 2 * P)
-
         def node_regroup(q):
-            node_grouped[q] = short.tile([P, 2, P, PACK], BF16, name="node_grouped", align_bytes=64)
-            rows = half_of("tx1", q)[:, :, window_of(q)].rearrange("p t (m e) -> p e m t", e=2)
+            if q % 2 == 0:
+                node_grouped[q // 2] = short.tile([P, 2, 2, P, PACK], BF16, name="node_grouped", align_bytes=64)
+            j = q % HALF
+            rows = half_of("tx1", q)[:, :, j * 2 * P : (j + 1) * 2 * P].rearrange("p t (m e) -> p e m t", e=2)
             if q < HALF:
-                nc.vector.tensor_copy(out=node_grouped[q][:], in_=rows)
+                nc.vector.tensor_copy(out=node_grouped[q // 2][:, q % 2], in_=rows)
             else:
-                nc.scalar.copy(out=node_grouped[q][:], in_=rows)
+                nc.scalar.copy(out=node_grouped[q // 2][:, q % 2], in_=rows)
 
         def node_quantise(q):
             key = (q // CHUNKS, (q % CHUNKS) // HALF)
-            if q % HALF == 0:
+            if q % HALF == 1:
                 node_codes[key] = (
                     node_pool.tile([P, FEATS], U32, name="node_c", align_bytes=64),
                     node_pool.tile([P, FEATS], U8, name="node_s", align_bytes=64),
                 )
             codes, scales = node_codes[key]
+            windows = slice((q % HALF - 1) * 2 * P, (q % HALF + 1) * 2 * P)
             nc.vector.quantize_mx(
-                out=codes[:, window_of(q)].bitcast(FP8X4),
-                scales=scales[:, window_of(q)],
-                in_=node_grouped[q][:].rearrange("p e m t -> p (e m t)"),
+                out=codes[:, windows].bitcast(FP8X4),
+                scales=scales[:, windows],
+                in_=node_grouped[q // 2][:].rearrange("p w e m t -> p (w e m t)"),
             )
 
         def row_sums(q):
@@ -223,7 +223,12 @@ def tile_cheblayer_pb_t_kernel(tc, x, tx1, adj, W, b, out):
                     in_=spread[:].rearrange("p (c e) n -> p c n e", e=2),
                 )
 
-        chunks = {s: {} for s in range(ALL_CHUNKS)}
+        chunks = {s: {} for s in range(ALL_CHUNKS + TX2_LAG)}
+
+        def grouped_of(s):
+            if "grouped" not in chunks[s]:
+                chunks[s]["grouped"] = grouped_pool.tile([P, 4, PASSES, P, PACK], BF16, name="grouped", align_bytes=64)
+            return chunks[s]["grouped"]
 
         def transposed_words(src_half, j):
             words = src_half[:].bitcast(F32)
@@ -233,21 +238,20 @@ def tile_cheblayer_pb_t_kernel(tc, x, tx1, adj, W, b, out):
             return bank
 
         def feat_transpose(s):
-            t = chunks[s]
-            t["feat_grouped"] = long.tile([P, 2, PASSES, P, PACK], BF16, name="feat_grouped", align_bytes=64)
-            feat_words = t["feat_grouped"][:].bitcast(F32)
-            for m, name in enumerate(("x", "tx1")):
+            words = grouped_of(s)[:].bitcast(F32)
+            for section, name in ((X, "x"), (TX1, "tx1")):
                 bank = transposed_words(half_of(name, s), s % HALF)
-                nc.scalar.copy(out=feat_words[:, m], in_=bank[:].rearrange("p (a u) i -> p a i u", u=2))
+                nc.scalar.copy(out=words[:, section], in_=bank[:].rearrange("p (a u) i -> p a i u", u=2))
 
-        def feat_quantise(s):
+        def quantise(s, first, last):
             t = chunks[s]
-            t["feat_c"] = long.tile([P, 2, PASSES, P], U32, name="feat_c", align_bytes=64)
-            t["feat_s"] = long.tile([P, 2, PASSES, P], U8, name="feat_s", align_bytes=64)
+            if "codes" not in t:
+                t["codes"] = codes_pool.tile([P, 4, PASSES, P], U32, name="codes", align_bytes=64)
+                t["scales"] = codes_pool.tile([P, 4, PASSES, P], U8, name="scales", align_bytes=64)
             nc.vector.quantize_mx(
-                out=t["feat_c"][:].rearrange("p m a i -> p (m a i)").bitcast(FP8X4),
-                scales=t["feat_s"][:].rearrange("p m a i -> p (m a i)"),
-                in_=t["feat_grouped"][:].rearrange("p m a i t -> p (m a i t)"),
+                out=t["codes"][:, first:last].rearrange("p m a i -> p (m a i)").bitcast(FP8X4),
+                scales=t["scales"][:, first:last].rearrange("p m a i -> p (m a i)"),
+                in_=t["grouped"][:, first:last].rearrange("p m a i t -> p (m a i t)"),
             )
 
         def lap_rows(s):
@@ -262,35 +266,20 @@ def tile_cheblayer_pb_t_kernel(tc, x, tx1, adj, W, b, out):
             k = s % CHUNKS
             row = half_of("adj", s)[:, s % HALF, :]
             diag_cols = row.rearrange("p (w n e) -> p w n e", n=P, e=2)[:, k // 2, :, k % 2]
-            eye = short.tile([P, P], F32, name="eye")
-            nc.gpsimd.tensor_scalar(
-                out=eye[:],
+            nc.vector.scalar_tensor_tensor(
+                out=diag_cols,
                 in0=ident[:],
-                scalar1=vectors[s // CHUNKS]["eye_fix"][:, k : k + 1],
-                scalar2=0.0,
+                scalar=vectors[s // CHUNKS]["eye_fix"][:, k : k + 1],
+                in1=diag_cols,
                 op0=ALU.mult,
                 op1=ALU.add,
             )
-            nc.gpsimd.tensor_tensor(out=diag_cols, in0=diag_cols, in1=eye[:], op=ALU.add)
 
         def lap_transpose(s):
             bank = transposed_words(half_of("adj", s), s % HALF)
             pairs = bank[:].bitcast(BF16).rearrange("p (a u) (i e) -> p a i u e", u=2, e=2)
-            chunks[s]["lap_grouped"] = short.tile([P, PASSES, P, PACK], BF16, name="lap_grouped", align_bytes=64)
             for a in range(PASSES):
-                nc.scalar.copy(
-                    out=chunks[s]["lap_grouped"][:, a].rearrange("p i (u e) -> p i u e", e=2), in_=pairs[:, a]
-                )
-
-        def lap_quantise(s):
-            t = chunks[s]
-            t["lap_c"] = short.tile([P, PASSES, P], U32, name="lap_c", align_bytes=64)
-            t["lap_s"] = short.tile([P, PASSES, P], U8, name="lap_s", align_bytes=64)
-            nc.vector.quantize_mx(
-                out=t["lap_c"][:].rearrange("p a i -> p (a i)").bitcast(FP8X4),
-                scales=t["lap_s"][:].rearrange("p a i -> p (a i)"),
-                in_=t["lap_grouped"][:].rearrange("p a i t -> p (a i t)"),
-            )
+                nc.scalar.copy(out=grouped_of(s)[:, LAP, a].rearrange("p i (u e) -> p i u e", e=2), in_=pairs[:, a])
 
         def second_order_products(s):
             t = chunks[s]
@@ -306,33 +295,20 @@ def tile_cheblayer_pb_t_kernel(tc, x, tx1, adj, W, b, out):
                             out=acc[:, v, :],
                             lhsT=codes[:, cols].bitcast(FP8X4),
                             lhsT_scale=scales[:, cols],
-                            rhs=t["lap_c"][:, h, :].bitcast(FP8X4),
-                            rhs_scale=t["lap_s"][:, h, :],
+                            rhs=t["codes"][:, LAP, h, :].bitcast(FP8X4),
+                            rhs_scale=t["scales"][:, LAP, h, :],
                             start=(h == 0),
                             stop=(h == PASSES - 1),
                         )
 
         def second_order_term(s, a):
-            t = chunks[s]
-            if a == 0:
-                t["tx2_grouped"] = short.tile([P, PASSES, P, PACK], BF16, name="tx2_grouped", align_bytes=64)
             nc.vector.scalar_tensor_tensor(
-                out=t["tx2_grouped"][:, a],
-                in0=t["acc"][a][:].rearrange("p v i -> p i v"),
+                out=grouped_of(s + TX2_LAG)[:, TX2, a],
+                in0=chunks[s]["acc"][a][:].rearrange("p v i -> p i v"),
                 scalar=2.0,
-                in1=t["feat_grouped"][:, 0, a],
+                in1=grouped_of(s)[:, X, a],
                 op0=ALU.mult,
                 op1=ALU.subtract,
-            )
-
-        def tx2_quantise(s):
-            t = chunks[s]
-            t["tx2_c"] = short.tile([P, PASSES, P], U32, name="tx2_c", align_bytes=64)
-            t["tx2_s"] = short.tile([P, PASSES, P], U8, name="tx2_s", align_bytes=64)
-            nc.vector.quantize_mx(
-                out=t["tx2_c"][:].rearrange("p a i -> p (a i)").bitcast(FP8X4),
-                scales=t["tx2_s"][:].rearrange("p a i -> p (a i)"),
-                in_=t["tx2_grouped"][:].rearrange("p a i t -> p (a i t)"),
             )
 
         pair_acc = {}
@@ -341,10 +317,11 @@ def tile_cheblayer_pb_t_kernel(tc, x, tx1, adj, W, b, out):
             t = chunks[s]
             if s % 2 == 0:
                 pair_acc[s // 2] = psum_o.tile([P, 2, P], F32, name="out_acc")
+            later = chunks[s + TX2_LAG]
             operands = [
-                (t["feat_c"][:, 0], t["feat_s"][:, 0]),
-                (t["feat_c"][:, 1], t["feat_s"][:, 1]),
-                (t["tx2_c"][:], t["tx2_s"][:]),
+                (t["codes"][:, X], t["scales"][:, X]),
+                (t["codes"][:, TX1], t["scales"][:, TX1]),
+                (later["codes"][:, TX2], later["scales"][:, TX2]),
             ]
             for k, (codes, scales) in enumerate(operands):
                 for a in range(PASSES):
@@ -369,7 +346,7 @@ def tile_cheblayer_pb_t_kernel(tc, x, tx1, adj, W, b, out):
                 nc.tensor.transpose(out=bank[:, e, :], in_=chunks[s]["relu"][:, e, :], identity=ident[:])
             result = short.tile([P, 2, OUT], F32, name="result")
             nc.scalar.copy(out=result[:], in_=bank[:])
-            nc.gpsimd.dma_start(
+            nc.sync.dma_start(
                 out=out[g, c * 2 * P : (c + 1) * 2 * P, :].rearrange("(p e) o -> p e o", e=2), in_=result[:]
             )
 
@@ -409,13 +386,12 @@ def tile_cheblayer_pb_t_kernel(tc, x, tx1, adj, W, b, out):
 
             if valid(n + AT_OUTPUT):
                 output_products(n + AT_OUTPUT)
+            if valid(lap_side(n + AT_ROW_SUMS)):
+                row_sums(lap_side(n + AT_ROW_SUMS))
             if second_of_pair(n + AT_STORE):
                 output_store(n + AT_STORE)
             if valid(n + AT_TRANSPOSE):
                 feat_transpose(n + AT_TRANSPOSE)
-            if valid(lap_side(n + AT_ROW_SUMS)):
-                row_sums(lap_side(n + AT_ROW_SUMS))
-            if valid(n + AT_TRANSPOSE):
                 lap_transpose(n + AT_TRANSPOSE)
 
             if n + AT_QUANTISE == 0:
@@ -424,20 +400,20 @@ def tile_cheblayer_pb_t_kernel(tc, x, tx1, adj, W, b, out):
                 vectors_reciprocal(lap_side(n + AT_RECIPROCAL) // CHUNKS)
             if valid(lap_side(n + AT_LAP)):
                 lap_rows(lap_side(n + AT_LAP))
-            if valid(n + AT_QUANTISE):
-                lap_quantise(n + AT_QUANTISE)
             if valid(n + AT_TERM):
                 second_order_term(n + AT_TERM, 0)
                 second_order_term(n + AT_TERM, 1)
-            if valid(n + AT_QUANTISE):
-                feat_quantise(n + AT_QUANTISE)
-            if valid(n + AT_TERM):
-                tx2_quantise(n + AT_TERM)
-            if valid(n + AT_NODE_QUANTISE):
+            if valid(lap_side(n + AT_LAP)):
+                lap_add_eye(lap_side(n + AT_LAP))
+            if valid(n + AT_QUANTISE) and valid(n + AT_TERM):
+                quantise(n + AT_QUANTISE, X, TX2 + 1)
+            elif valid(n + AT_QUANTISE):
+                quantise(n + AT_QUANTISE, X, TX1 + 1)
+                quantise(n + AT_QUANTISE, LAP, LAP + 1)
+            elif valid(n + AT_TERM):
+                quantise(n + AT_QUANTISE, TX2, TX2 + 1)
+            if second_of_pair(n + AT_NODE_QUANTISE):
                 node_quantise(n + AT_NODE_QUANTISE)
-
-            if valid(lap_side(n + AT_EYE)):
-                lap_add_eye(lap_side(n + AT_EYE))
 
             if valid(n + AT_SECOND_ORDER):
                 second_order_products(n + AT_SECOND_ORDER)

from contextlib import ExitStack

import concourse.mybir as mybir
from concourse.masks import make_identity

F32 = mybir.dt.float32
BF16 = mybir.dt.bfloat16
U32 = mybir.dt.uint32
U8 = mybir.dt.uint8
FP8X4 = mybir.dt.float8_e4m3fn_x4
ALU = mybir.AluOpType
ACT = mybir.ActivationFunctionType

P = 128
GRAPHS = 4
NODES = 1024
FEATS = 1024
OUT = 128
ORDERS = 3
EPS = 1e-6

BLOCK_BF16 = 16
PACK = 4
K_PASS = P * PACK
PASSES = NODES // K_PASS
CHUNKS = NODES // P
HALF = CHUNKS // PASSES
ALL_CHUNKS = GRAPHS * CHUNKS

AT_STORE = -1
AT_RELU = 0
AT_OUTPUT = 1
AT_TERM = 2
AT_SECOND_ORDER = 3
AT_QUANTISE = 4
AT_TRANSPOSE = 5
AT_LAP = 8
AT_SPREAD = AT_LAP + 1
AT_RECIPROCAL = AT_LAP + 2
AT_ROOT = AT_LAP + 3
AT_ROW_SUMS = AT_ROOT + CHUNKS
AT_NODE_QUANTISE = AT_SECOND_ORDER + 1 + CHUNKS
AT_NODE_REGROUP = AT_NODE_QUANTISE + 1
X, TX1, LAP, TX2 = 0, 1, 2, 3
TX2_LAG = AT_QUANTISE - AT_TERM
EARLY = 4
LOAD_AHEAD = 4
ADJ_BUFS = 6
TX1_BUFS = 4
X_BUFS = 2
assert AT_ROW_SUMS + LOAD_AHEAD <= AT_TRANSPOSE + (ADJ_BUFS - 1) * HALF
assert AT_NODE_REGROUP + LOAD_AHEAD <= AT_TRANSPOSE + (TX1_BUFS - 1) * HALF
assert AT_TRANSPOSE + LOAD_AHEAD <= AT_TRANSPOSE + (X_BUFS - 1) * HALF

FLOPS = GRAPHS * (2 * NODES * NODES * FEATS + ORDERS * 2 * NODES * FEATS * OUT)


def tile_cheblayer_pb_t_kernel(tc, x, tx1, adj, W, b, out):
    nc = tc.nc
    with ExitStack() as stack:
        pool = lambda name, bufs: stack.enter_context(tc.tile_pool(name=name, bufs=bufs))
        const = pool("const", 1)
        adj_pool = pool("adj", ADJ_BUFS)
        tx1_pool = pool("tx1", TX1_BUFS)
        x_pool = pool("x", X_BUFS)
        graph_pool = pool("graph", 3)
        node_pool = pool("node", 5)
        short = pool("short", 3)
        grouped_pool = pool("grouped", 5)
        codes_pool = pool("codes", 4)
        psum_t = stack.enter_context(tc.psum_pool(name="psum_t", bufs=4))
        psum_m = stack.enter_context(tc.psum_pool(name="psum_m", bufs=2))
        psum_o = stack.enter_context(tc.psum_pool(name="psum_o", bufs=2))
        stack.enter_context(tc.manual_schedule())

        ident = const.tile([P, P], F32)
        make_identity(nc, ident[:])
        ident_bf = const.tile([P, P], BF16)
        make_identity(nc, ident_bf[:])
        eps = const.tile([P, 1], F32)
        nc.vector.memset(eps[:], EPS)
        warm = const.tile([P, 1], F32)
        nc.scalar.activation(out=warm[:], in_=eps[:], func=ACT.Sqrt)

        halves = {}

        def load_half(name, src, tile_pool, q):
            g, h = q // CHUNKS, (q % CHUNKS) // HALF
            t = tile_pool.tile([P, HALF, FEATS], BF16, name=name)
            rows = src[g, h * K_PASS : (h + 1) * K_PASS, :].rearrange("(c p e) f -> c p e f", p=P, e=2)
            for c in range(HALF // 2):
                nc.sync.dma_start(out=t[:, 2 * c : 2 * c + 2, :], in_=rows[c])
            halves[(name, g, h)] = t

        def half_of(name, s):
            return halves[(name, s // CHUNKS, (s % CHUNKS) // HALF)]

        w_raw = const.tile([P, ORDERS * PASSES, PACK, OUT], BF16)
        w_grouped = const.tile([P, ORDERS * PASSES, OUT, PACK], BF16, align_bytes=64)
        w_codes = const.tile([P, ORDERS, PASSES, OUT], U32, align_bytes=64)
        w_scales = const.tile([P, ORDERS, PASSES, OUT], U8, align_bytes=64)
        b_rows = const.tile([P, P], BF16)
        b_terms = const.tile([P, ORDERS], F32)
        bias = const.tile([P, 1], F32)

        def load_weights():
            nc.sync.dma_start(
                out=w_raw[:].rearrange("p a (u e) o -> p (a u) e o", e=2),
                in_=W.rearrange("k (a p e) o -> p (k a) e o", p=P, e=2),
            )
            nc.vector.memset(b_rows[:], 0.0)
            nc.sync.dma_start(out=b_rows[0:ORDERS, :], in_=b)

        def quantise_weights():
            nc.vector.tensor_copy(out=w_grouped[:], in_=w_raw[:].rearrange("p a t o -> p a o t"))
            for k in range(ORDERS):
                nc.vector.quantize_mx(
                    out=w_codes[:, k].rearrange("p a o -> p (a o)").bitcast(FP8X4),
                    scales=w_scales[:, k].rearrange("p a o -> p (a o)"),
                    in_=w_grouped[:, k * PASSES : (k + 1) * PASSES].rearrange("p a o t -> p (a o t)"),
                )
            b_cols = psum_t.tile([P, P], BF16, name="bank")
            nc.tensor.transpose(out=b_cols[:], in_=b_rows[:], identity=ident_bf[:])
            nc.scalar.activation(out=b_terms[:], in_=b_cols[:, 0:ORDERS], func=ACT.Copy, accum_out=bias[:, 0:1])

        vectors = {g: {} for g in range(GRAPHS)}
        node_codes = {}
        node_grouped = {}

        def node_regroup(q):
            if q % 2 == 0:
                node_grouped[q // 2] = short.tile([P, 2, 2, P, PACK], BF16, name="node_grouped", align_bytes=64)
            j = q % HALF
            rows = half_of("tx1", q)[:, :, j * 2 * P : (j + 1) * 2 * P].rearrange("p t (m e) -> p e m t", e=2)
            if q < HALF:
                nc.vector.tensor_copy(out=node_grouped[q // 2][:, q % 2], in_=rows)
            else:
                nc.scalar.copy(out=node_grouped[q // 2][:, q % 2], in_=rows)

        def node_quantise(q):
            key = (q // CHUNKS, (q % CHUNKS) // HALF)
            if q % HALF == 1:
                node_codes[key] = (
                    node_pool.tile([P, FEATS], U32, name="node_c", align_bytes=64),
                    node_pool.tile([P, FEATS], U8, name="node_s", align_bytes=64),
                )
            codes, scales = node_codes[key]
            windows = slice((q % HALF - 1) * 2 * P, (q % HALF + 1) * 2 * P)
            nc.vector.quantize_mx(
                out=codes[:, windows].bitcast(FP8X4),
                scales=scales[:, windows],
                in_=node_grouped[q // 2][:].rearrange("p w e m t -> p (w e m t)"),
            )

        def row_sums(q):
            g, k = q // CHUNKS, q % CHUNKS
            if k == 0:
                vectors[g]["d"] = graph_pool.tile([P, CHUNKS], F32, name="d")
            folded = psum_t.tile([P, P], F32, name="bank")
            for blk in range(CHUNKS):
                nc.tensor.matmul(
                    out=folded[:],
                    lhsT=ident_bf[:],
                    rhs=half_of("adj", q)[:, q % HALF, blk * P : (blk + 1) * P],
                    start=(blk == 0),
                    stop=(blk == CHUNKS - 1),
                )
            junk = short.tile([P, P], F32, name="junk")
            nc.scalar.activation(out=junk[:], in_=folded[:], func=ACT.Copy, accum_out=vectors[g]["d"][:, k : k + 1])

        def vectors_root(g):
            vectors[g]["root"] = graph_pool.tile([P, CHUNKS], F32, name="root")
            nc.scalar.activation(out=vectors[g]["root"][:], in_=vectors[g]["d"][:], func=ACT.Sqrt, bias=eps[:, 0:1])

        def vectors_reciprocal(g):
            v = vectors[g]
            v["r"] = graph_pool.tile([P, CHUNKS], F32, name="r")
            nc.vector.reciprocal(out=v["r"][:], in_=v["root"][:])
            v["neg_r"] = graph_pool.tile([P, CHUNKS], F32, name="neg_r")
            nc.vector.tensor_scalar_mul(out=v["neg_r"][:], in0=v["r"][:], scalar1=-1.0)

        def load_diagonal(g):
            vectors[g]["a_diag"] = graph_pool.tile([P, 2, BLOCK_BF16], BF16, name="a_diag")
            diagonal = adj[g].rearrange("i j -> (i j)")[0 : NODES * NODES : NODES + 1]
            with nc.allow_non_contiguous_dma(reason="1,024 single elements, one from each row of adj"):
                for e in range(2):
                    nc.sync.dma_start(
                        out=vectors[g]["a_diag"][:, e, 0 : CHUNKS // 2],
                        in_=diagonal.rearrange("(c p e) -> p c e", p=P, e=2)[:, :, e],
                    )

        def vectors_diagonal(g):
            v = vectors[g]
            small = lambda name, dtype: graph_pool.tile([P, CHUNKS], dtype, name=name)
            half_product, product, stored, one_more = (
                small("half_product", F32), small("product", F32), small("stored", BF16), small("one_more", F32)
            )
            v["eye_fix"] = small("eye_fix", F32)
            by_pair = lambda ap: ap.rearrange("p (c e) -> p c e", e=2)
            nc.gpsimd.tensor_tensor(
                out=by_pair(half_product[:]),
                in0=v["a_diag"][:, :, 0 : CHUNKS // 2].rearrange("p e c -> p c e"),
                in1=by_pair(v["neg_r"][:]),
                op=ALU.mult,
            )
            nc.gpsimd.tensor_tensor(out=product[:], in0=half_product[:], in1=v["r"][:], op=ALU.mult)
            nc.gpsimd.tensor_copy(out=stored[:], in_=product[:])
            nc.gpsimd.tensor_scalar_add(out=one_more[:], in0=product[:], scalar1=1.0)
            nc.gpsimd.tensor_tensor(out=v["eye_fix"][:], in0=one_more[:], in1=stored[:], op=ALU.subtract)

        def vectors_spread(g):
            v = vectors[g]
            v["r_cols"] = graph_pool.tile([P, NODES], F32, name="r_cols")
            for h in range(PASSES):
                spread = psum_t.tile([P, HALF, P], F32, name="bank")
                for j in range(HALF):
                    k = h * HALF + j
                    nc.tensor.transpose(
                        out=spread[:, j, :], in_=v["r"][:, k : k + 1].to_broadcast([P, P]), identity=ident[:]
                    )
                nc.scalar.copy(
                    out=v["r_cols"][:, h * K_PASS : (h + 1) * K_PASS].rearrange("p (c n e) -> p c n e", n=P, e=2),
                    in_=spread[:].rearrange("p (c e) n -> p c n e", e=2),
                )

        chunks = {s: {} for s in range(ALL_CHUNKS + TX2_LAG)}

        def grouped_of(s):
            if "grouped" not in chunks[s]:
                chunks[s]["grouped"] = grouped_pool.tile([P, 4, PASSES, P, PACK], BF16, name="grouped", align_bytes=64)
            return chunks[s]["grouped"]

        def transposed_words(src_half, j):
            words = src_half[:].bitcast(F32)
            bank = psum_t.tile([P, PACK, P], F32, name="bank")
            for u in range(PACK):
                nc.tensor.transpose(out=bank[:, u, :], in_=words[:, j, u * P : (u + 1) * P], identity=ident[:])
            return bank

        def feat_transpose(s):
            words = grouped_of(s)[:].bitcast(F32)
            for section, name in ((X, "x"), (TX1, "tx1")):
                bank = transposed_words(half_of(name, s), s % HALF)
                nc.scalar.copy(out=words[:, section], in_=bank[:].rearrange("p (a u) i -> p a i u", u=2))

        def quantise(s, first, last):
            t = chunks[s]
            if "codes" not in t:
                t["codes"] = codes_pool.tile([P, 4, PASSES, P], U32, name="codes", align_bytes=64)
                t["scales"] = codes_pool.tile([P, 4, PASSES, P], U8, name="scales", align_bytes=64)
            nc.vector.quantize_mx(
                out=t["codes"][:, first:last].rearrange("p m a i -> p (m a i)").bitcast(FP8X4),
                scales=t["scales"][:, first:last].rearrange("p m a i -> p (m a i)"),
                in_=t["grouped"][:, first:last].rearrange("p m a i t -> p (m a i t)"),
            )

        def lap_rows(s):
            k = s % CHUNKS
            v = vectors[s // CHUNKS]
            row = half_of("adj", s)[:, s % HALF, :]
            nc.vector.scalar_tensor_tensor(
                out=row, in0=row, scalar=v["neg_r"][:, k : k + 1], in1=v["r_cols"][:], op0=ALU.mult, op1=ALU.mult
            )

        def lap_add_eye(s):
            k = s % CHUNKS
            row = half_of("adj", s)[:, s % HALF, :]
            diag_cols = row.rearrange("p (w n e) -> p w n e", n=P, e=2)[:, k // 2, :, k % 2]
            nc.vector.scalar_tensor_tensor(
                out=diag_cols,
                in0=ident[:],
                scalar=vectors[s // CHUNKS]["eye_fix"][:, k : k + 1],
                in1=diag_cols,
                op0=ALU.mult,
                op1=ALU.add,
            )

        def lap_transpose(s):
            bank = transposed_words(half_of("adj", s), s % HALF)
            pairs = bank[:].bitcast(BF16).rearrange("p (a u) (i e) -> p a i u e", u=2, e=2)
            for a in range(PASSES):
                nc.scalar.copy(out=grouped_of(s)[:, LAP, a].rearrange("p i (u e) -> p i u e", e=2), in_=pairs[:, a])

        def second_order_products(s):
            t = chunks[s]
            t["acc"] = []
            for a in range(PASSES):
                acc = psum_m.tile([P, PACK, P], F32, name="acc")
                t["acc"].append(acc)
                for v in range(PACK):
                    cols = slice((a * PACK + v) * P, (a * PACK + v + 1) * P)
                    for h in range(PASSES):
                        codes, scales = node_codes[(s // CHUNKS, h)]
                        nc.tensor.matmul_mx(
                            out=acc[:, v, :],
                            lhsT=codes[:, cols].bitcast(FP8X4),
                            lhsT_scale=scales[:, cols],
                            rhs=t["codes"][:, LAP, h, :].bitcast(FP8X4),
                            rhs_scale=t["scales"][:, LAP, h, :],
                            start=(h == 0),
                            stop=(h == PASSES - 1),
                        )

        def second_order_term(s, a):
            nc.vector.scalar_tensor_tensor(
                out=grouped_of(s + TX2_LAG)[:, TX2, a],
                in0=chunks[s]["acc"][a][:].rearrange("p v i -> p i v"),
                scalar=2.0,
                in1=grouped_of(s)[:, X, a],
                op0=ALU.mult,
                op1=ALU.subtract,
            )

        pair_acc = {}

        def output_products(s):
            t = chunks[s]
            if s % 2 == 0:
                pair_acc[s // 2] = psum_o.tile([P, 2, P], F32, name="out_acc")
            later = chunks[s + TX2_LAG]
            operands = [
                (t["codes"][:, X], t["scales"][:, X]),
                (t["codes"][:, TX1], t["scales"][:, TX1]),
                (later["codes"][:, TX2], later["scales"][:, TX2]),
            ]
            for k, (codes, scales) in enumerate(operands):
                for a in range(PASSES):
                    nc.tensor.matmul_mx(
                        out=pair_acc[s // 2][:, s % 2, :],
                        lhsT=w_codes[:, k, a, :].bitcast(FP8X4),
                        lhsT_scale=w_scales[:, k, a, :],
                        rhs=codes[:, a, :].bitcast(FP8X4),
                        rhs_scale=scales[:, a, :],
                        start=(k == 0 and a == 0),
                        stop=(k == ORDERS - 1 and a == PASSES - 1),
                    )

        def output_relu(s):
            chunks[s]["relu"] = short.tile([P, 2, P], F32, name="relu")
            nc.scalar.activation(out=chunks[s]["relu"][:], in_=pair_acc[s // 2][:], func=ACT.Relu, bias=bias[:, 0:1])

        def output_store(s):
            g, c = s // CHUNKS, (s % CHUNKS) // 2
            bank = psum_t.tile([P, 2, OUT], F32, name="bank")
            for e in range(2):
                nc.tensor.transpose(out=bank[:, e, :], in_=chunks[s]["relu"][:, e, :], identity=ident[:])
            result = short.tile([P, 2, OUT], F32, name="result")
            nc.scalar.copy(out=result[:], in_=bank[:])
            nc.sync.dma_start(
                out=out[g, c * 2 * P : (c + 1) * 2 * P, :].rearrange("(p e) o -> p e o", e=2), in_=result[:]
            )

        valid = lambda s: 0 <= s < ALL_CHUNKS
        first_of_half = lambda s: valid(s) and s % HALF == 0
        first_of_graph = lambda s: valid(s) and s % CHUNKS == 0
        second_of_pair = lambda s: valid(s) and s % 2 == 1

        def lap_side(m):
            if m + EARLY < CHUNKS:
                return m + EARLY
            return m if m >= CHUNKS else -1

        first_step = -(AT_ROW_SUMS + LOAD_AHEAD + EARLY)
        for n in range(first_step, ALL_CHUNKS - AT_STORE):
            if first_of_half(n + AT_TRANSPOSE + LOAD_AHEAD):
                load_half("x", x, x_pool, n + AT_TRANSPOSE + LOAD_AHEAD)
            if n + AT_TRANSPOSE + LOAD_AHEAD == 0:
                load_weights()
            if first_of_half(n + AT_NODE_REGROUP + LOAD_AHEAD):
                load_half("tx1", tx1, tx1_pool, n + AT_NODE_REGROUP + LOAD_AHEAD)
            if first_of_half(lap_side(n + AT_ROW_SUMS + LOAD_AHEAD)):
                load_half("adj", adj, adj_pool, lap_side(n + AT_ROW_SUMS + LOAD_AHEAD))
            if first_of_graph(lap_side(n + AT_ROW_SUMS)):
                load_diagonal(lap_side(n + AT_ROW_SUMS) // CHUNKS)

            if first_of_graph(lap_side(n + AT_ROOT)):
                vectors_root(lap_side(n + AT_ROOT) // CHUNKS)
            if first_of_graph(lap_side(n + AT_SPREAD)):
                vectors_spread(lap_side(n + AT_SPREAD) // CHUNKS)
                vectors_diagonal(lap_side(n + AT_SPREAD) // CHUNKS)

            if second_of_pair(n + AT_RELU):
                output_relu(n + AT_RELU)
            if valid(n + AT_NODE_REGROUP):
                node_regroup(n + AT_NODE_REGROUP)

            if valid(n + AT_OUTPUT):
                output_products(n + AT_OUTPUT)
            if valid(lap_side(n + AT_ROW_SUMS)):
                row_sums(lap_side(n + AT_ROW_SUMS))
            if second_of_pair(n + AT_STORE):
                output_store(n + AT_STORE)
            if valid(n + AT_TRANSPOSE):
                feat_transpose(n + AT_TRANSPOSE)
                lap_transpose(n + AT_TRANSPOSE)

            if n + AT_QUANTISE == 0:
                quantise_weights()
            if first_of_graph(lap_side(n + AT_RECIPROCAL)):
                vectors_reciprocal(lap_side(n + AT_RECIPROCAL) // CHUNKS)
            if valid(lap_side(n + AT_LAP)):
                lap_rows(lap_side(n + AT_LAP))
            if valid(n + AT_TERM):
                second_order_term(n + AT_TERM, 0)
                second_order_term(n + AT_TERM, 1)
            if valid(lap_side(n + AT_LAP)):
                lap_add_eye(lap_side(n + AT_LAP))
            if valid(n + AT_QUANTISE) and valid(n + AT_TERM):
                quantise(n + AT_QUANTISE, X, TX2 + 1)
            elif valid(n + AT_QUANTISE):
                quantise(n + AT_QUANTISE, X, TX1 + 1)
                quantise(n + AT_QUANTISE, LAP, LAP + 1)
            elif valid(n + AT_TERM):
                quantise(n + AT_QUANTISE, TX2, TX2 + 1)
            if second_of_pair(n + AT_NODE_QUANTISE):
                node_quantise(n + AT_NODE_QUANTISE)

            if valid(n + AT_SECOND_ORDER):
                second_order_products(n + AT_SECOND_ORDER)
